import numpy as np
import ml_dtypes


def mxq(x, axis, fmt="e4m3"):
    dtype, down = {"e4m3": (ml_dtypes.float8_e4m3fn, 7), "e5m2": (ml_dtypes.float8_e5m2, 14)}[fmt]
    v = np.moveaxis(np.asarray(x, np.float32).astype(ml_dtypes.bfloat16).astype(np.float64), axis, -1)
    blocks = v.reshape(v.shape[:-1] + (-1, 32))
    amax = np.abs(blocks).max(-1, keepdims=True)
    byte = np.maximum(np.where(amax > 0, np.frexp(amax)[1] - 1 + 127, 0) - down, 1)
    scale = np.exp2(byte - 127.0)
    codes = (blocks / scale).astype(np.float32).astype(dtype).astype(np.float64)
    return np.moveaxis((codes * scale).reshape(v.shape), -1, axis)


WIDE = False


def mx_kscale(k):
    if not WIDE:
        return np.ones(k)
    levels = np.array([18, -18])
    if k % 512:
        return np.exp2(np.random.permutation(np.resize(levels, k // 32))).repeat(32)
    a = np.empty((k // 512, 16))
    for p in range(k // 512):
        a[p, :8] = np.random.permutation(np.resize(levels, 8))
        for g in range(8):
            far = levels[np.abs(levels - a[p, g]) >= 10]
            a[p, g + 8] = far[np.random.randint(len(far))]
    return np.exp2(a.ravel()).repeat(32)


BF16 = ml_dtypes.bfloat16


def bf(x):
    return np.asarray(x, np.float32).astype(BF16)


def f64(x):
    return np.asarray(x).astype(np.float64)


B, T, E, H, KV = 2, 512, 1280, 10, 1
HD = E // H
N = B * T
J = (H + 2 * KV) * HD
ROPE_BASE = 10000.0


def rotate_half(t):
    d = t.shape[-1] // 2
    return np.concatenate([-t[..., d:], t[..., :d]], axis=-1)


def rope_tables():
    pos = ROPE_BASE ** ((-2.0 * np.arange(0, HD, 2) - 1.0) / HD)
    angles = np.arange(T)[:, None] * pos[None, :]
    rot = np.concatenate([angles, angles], axis=-1)
    return np.cos(rot), np.sin(rot)


def rope_back(g, cos, sin):
    return g * cos - rotate_half(g * sin)


def to_rows(g):
    return g.transpose(0, 2, 1, 3).reshape(N, -1)


def setup_inputs():
    s = mx_kscale(N)
    u = mx_kscale(J).reshape(H + 2 * KV, HD)
    ur = np.concatenate([u[:, : HD // 2], u[:, : HD // 2]], axis=1)
    u = np.concatenate([ur[: H + KV], u[H + KV :]], axis=0)
    st = s.reshape(B, 1, T, 1)
    x = bf(np.random.standard_normal((B, T, E)) * s.reshape(B, T, 1))
    w_attn = bf(np.random.standard_normal((E, J)) * 1.25 * E ** -0.5 / u.reshape(1, J))
    uq = u[:H].reshape(1, H, 1, HD)
    uk = u[H : H + KV].reshape(1, KV, 1, HD)
    uv = u[H + KV :].reshape(1, KV, 1, HD)
    grad_0 = bf(np.random.standard_normal((B, H, T, HD)) * np.exp2(np.random.randint(-6, 1, (B, 1, T, 1))) / st * uq)
    grad_1 = bf(np.random.standard_normal((B, KV, T, HD)) * np.exp2(np.random.randint(-6, 1, (B, 1, T, 1))) / st * uk)
    grad_2 = bf(np.random.standard_normal((B, KV, T, HD)) * np.exp2(np.random.randint(-6, 1, (B, 1, T, 1))) / st * uv)
    return {"x": x, "w_attn": w_attn, "grad_0": grad_0, "grad_1": grad_1, "grad_2": grad_2}


def reference(x, w_attn, grad_0, grad_1, grad_2):
    cos, sin = rope_tables()
    dq = rope_back(f64(grad_0), cos, sin)
    dk = rope_back(f64(grad_1), cos, sin)
    dv = f64(grad_2)
    dz = np.concatenate([to_rows(dq), to_rows(dk), to_rows(dv)], axis=1)
    xr = f64(x).reshape(N, E)
    dx = mxq(dz, 1, "e5m2") @ mxq(f64(w_attn), 1, "e4m3").T
    dw = mxq(xr, 0, "e4m3").T @ mxq(dz, 0, "e5m2")
    return dx.reshape(B, T, E), dw

@@ -1,0 +1,483 @@
+import math
+from contextlib import ExitStack
+
+import concourse.mybir as mybir
+from concourse.masks import make_identity
+
+B, T, E, H, HD = 2, 512, 1280, 10, 128
+J = (H + 2) * HD
+FLOPS = 2 * 2 * B * T * E * J
+
+F32 = mybir.dt.float32
+BF16 = mybir.dt.bfloat16
+I32 = mybir.dt.int32
+U32 = mybir.dt.uint32
+U8 = mybir.dt.uint8
+E4M3 = mybir.dt.float8_e4m3fn_x4
+E5M2 = mybir.dt.float8_e5m2_x4
+ALU = mybir.AluOpType
+ACT = mybir.ActivationFunctionType
+
+P = 128
+PACK = 4
+HALF = HD // 2
+NW = 512
+GROUPS = J // NW
+E_TILES = E // P
+X_PIECE = 256
+X_LOADS = ((0, 512), (512, 1024), (1024, 1280))
+OUT0_WINDOWS = ((0, 0), (512, 512), (768, 1024))
+ROUND = 1.5 * 2.0**23
+UNITS = (
+    [(b, (i, i + 1), (0,)) for b in range(B) for i in (0, 2)]
+    + [(0, (i,), (1, 2)) for i in range(PACK)]
+    + [(1, (i,), (1, 2)) for i in (0, 1)]
+    + [(1, (2, 3), (g,)) for g in (2, 1)]
+)
+G_UNITS = 11
+LOADS = "X00 F0 X10 W0 W1 X01 W2 W3 X11 F1 W4 W5 X02 X12 W6 W7 R0 W8 W9 R1"
+W_ORDER = [(p, g) for p in range(5) for g in range(3)]
+W_STEP = (3, 3, 3, 3, 3, 0, 0, 0, 0, 0, 0, 0, 0)
+S_STEP = (2, 2, 2, 2, 0, 0, 0, 0, 2, 2, 0, 0, 0)
+QW_STEP = (0, 2, 2, 2, 2, 3, 3, 3, 0, 0, 0, 0)
+BUDGET = (0, 0, 0, 2, 6, 12, 12, 12, 12, 12, 12, 12)
+AHEAD = 5
+RESERVE = 2
+TAIL_V = 2
+FILL_EVERY = 2
+TAIL_A = 12
+
+
+def tile_multiqueryattention_pa_v_kernel(tc, x, w_attn, grad_0, grad_1, grad_2, out_0, out_1):
+    nc = tc.nc
+
+    with ExitStack() as ctx:
+        keep = ctx.enter_context(tc.tile_pool(name="keep", bufs=1))
+        ring = ctx.enter_context(tc.tile_pool(name="ring", bufs=3))
+        psum = ctx.enter_context(tc.psum_pool(name="psum", bufs=1))
+        ctx.enter_context(tc.manual_schedule())
+
+        free_banks = list(range(1, 8))
+
+        def take_bank():
+            k = free_banks.pop(0)
+            return k, psum.tile([P, NW], F32, name="bank", tag="bank%d" % k)
+
+        g_first, g_rest, dz_first, dz_rest, x_raw, w_raw = {}, {}, {}, {}, {}, {}
+
+        def load_first(b):
+            g_first[b] = keep.tile([P, 4 * T], BF16, name="g_first%d" % b)
+            nc.sync.dma_start(
+                out=g_first[b][:].rearrange("p (h c) -> p h c", h=4),
+                in_=grad_0[b, 0:4].rearrange("h (p i) d -> p h (i d)", i=PACK),
+            )
+
+        def load_rest(b):
+            g_rest[b] = keep.tile([P, 7 * T], BF16, name="g_rest%d" % b)
+            nc.sync.dma_start(
+                out=g_rest[b][:, 0 : 6 * T].rearrange("p (h c) -> p h c", h=6),
+                in_=grad_0[b, 4:H].rearrange("h (p i) d -> p h (i d)", i=PACK),
+            )
+            nc.sync.dma_start(out=g_rest[b][:, 6 * T :], in_=grad_1[b, 0].rearrange("(p i) d -> p (i d)", i=PACK))
+            nc.sync.dma_start(
+                out=dz_rest[b][:].rearrange("p (i c) -> p i c", i=PACK)[:, :, 7 * HD :],
+                in_=grad_2[b, 0].rearrange("(p i) d -> p i d", i=PACK),
+            )
+
+        def load_x(b, c):
+            lo, hi = X_LOADS[c]
+            x_raw[b, c] = keep.tile([P, PACK, hi - lo], BF16, name="x_raw%d_%d" % (b, c))
+            nc.sync.dma_start(out=x_raw[b, c][:], in_=x[b].rearrange("(p i) e -> p i e", i=PACK)[:, :, lo:hi])
+
+        def load_w(r):
+            w_raw[r] = keep.tile([P, J], BF16, name="w_raw", tag="w_or_out", bufs=E_TILES)
+            nc.sync.dma_start(out=w_raw[r][:], in_=w_attn[r * P : (r + 1) * P, :])
+
+        for b in range(B):
+            dz_first[b] = keep.tile([P, PACK * NW], BF16, name="dz_first%d" % b, align_bytes=64)
+            dz_rest[b] = keep.tile([P, PACK * 2 * NW], BF16, name="dz_rest%d" % b, align_bytes=64)
+
+        for word in LOADS.split():
+            if word[0] == "F":
+                load_first(int(word[1]))
+            elif word[0] == "R":
+                load_rest(int(word[1]))
+            elif word[0] == "W":
+                load_w(int(word[1]))
+            else:
+                load_x(int(word[1]), int(word[2]))
+
+        ident = keep.tile([P, P], F32, name="ident")
+        pos = keep.tile([P, T], F32, name="pos")
+        make_identity(nc, ident[:])
+        nc.gpsimd.iota(pos[:], pattern=[[1, PACK], [PACK, P]], base=0, channel_multiplier=0, allow_small_or_imprecise_dtypes=True)
+
+        table = psum.tile([P, NW], F32, name="table", tag="bank0")
+
+        def build_table():
+            one = keep.tile([P, 1], F32, name="one")
+            phase = keep.tile([P, 1], F32, name="phase")
+            factors = keep.tile([P, 16], F32, name="factors")
+            freqs = keep.tile([P, HALF], F32, name="freqs")
+            picked = keep.tile([P, P], F32, name="picked")
+            freq = keep.tile([P, 1], F32, name="freq")
+            nc.vector.memset(one[:], 1.0)
+            nc.vector.memset(phase[0:HALF, :], 0.25)
+            nc.vector.memset(phase[HALF:P, :], 0.0)
+            for a in range(8):
+                coarse = 10000.0 ** (-32.0 * a / HD)
+                fine = 10000.0 ** (-(4.0 * a + 1.0) / HD) / (2.0 * math.pi)
+                nc.vector.tensor_scalar(factors[:, a : a + 1], one[:], coarse, None, ALU.mult)
+                nc.vector.tensor_scalar(factors[:, 8 + a : 9 + a], one[:], fine, None, ALU.mult)
+            nc.vector.tensor_tensor(
+                out=freqs[:].rearrange("p (a c) -> p a c", a=8),
+                in0=factors[:, 0:8].unsqueeze(2).to_broadcast([P, 8, 8]),
+                in1=factors[:, 8:16].unsqueeze(1).to_broadcast([P, 8, 8]),
+                op=ALU.mult,
+            )
+            nc.vector.scalar_tensor_tensor(
+                out=picked[:].rearrange("p (s j) -> p s j", s=2),
+                in0=ident[:].rearrange("p (s j) -> p s j", s=2),
+                scalar=1.0,
+                in1=freqs[:].unsqueeze(1).to_broadcast([P, 2, HALF]),
+                op0=ALU.mult,
+                op1=ALU.mult,
+                accum_out=freq[:],
+            )
+            halves = [slice(0, T // 2), slice(T // 2, T)]
+            turns = keep.tile([P, T], F32, name="turns")
+            whole = keep.tile([P, T], I32, name="whole")
+            rest = keep.tile([P, T], F32, name="rest")
+            for s in halves:
+                nc.vector.tensor_scalar(turns[:, s], pos[:, s], freq[:], phase[:], ALU.mult, ALU.add)
+            for s in halves:
+                nc.vector.tensor_scalar(whole[:, s], turns[:, s], ROUND, None, ALU.add)
+            for s in halves:
+                nc.vector.scalar_tensor_tensor(rest[:, s], whole[:, s], ROUND, turns[:, s], ALU.subtract, ALU.subtract)
+            for s in halves:
+                nc.scalar.activation(out=pos[:, s], in_=rest[:, s], func=ACT.Sin, scale=-2.0 * math.pi)
+            for i in range(PACK):
+                nc.tensor.transpose(table[:, i * P : (i + 1) * P], pos[:, i * P : (i + 1) * P], ident[:])
+
+        warm = keep.tile([P, 1], F32, name="warm")
+
+        products, turned, zf_codes, zf_scales, zt_codes, zt_scales = {}, {}, {}, {}, {}, {}
+        x_codes = [keep.tile([P, E], U32, name="x_codes%d" % b, align_bytes=64) for b in range(B)]
+        x_scales = [keep.tile([P, E], U8, name="x_scales%d" % b, align_bytes=64) for b in range(B)]
+        w_codes = [keep.tile([P, E], U32, name="w_codes%d" % g, align_bytes=64) for g in range(GROUPS)]
+        w_scales = [keep.tile([P, E], U8, name="w_scales%d" % g, align_bytes=64) for g in range(GROUPS)]
+
+        def copy_on(engine, out, in_):
+            if engine == "vector":
+                nc.vector.tensor_copy(out=out, in_=in_)
+            elif engine == "gpsimd":
+                nc.gpsimd.tensor_scalar(out, in_, 1.0, 0.0, ALU.mult, ALU.add)
+            else:
+                nc.scalar.copy(out=out, in_=in_)
+
+        def dz_rows(b, groups):
+            if groups[0] == 0:
+                return dz_first[b][:].rearrange("p (i c) -> p i c", i=PACK)
+            lo = (groups[0] - 1) * NW
+            return dz_rest[b][:].rearrange("p (i c) -> p i c", i=PACK)[:, :, lo : lo + NW * len(groups)]
+
+        def rotated_heads(groups):
+            return sum(3 if g == GROUPS - 1 else 4 for g in groups)
+
+        def multiply(u, part):
+            b, slots, groups = UNITS[u]
+            nh = rotated_heads(groups)
+            if groups[0] == 0:
+                heads = g_first[b][:].rearrange("p (h i d) -> p h i d", h=4, i=PACK)
+            else:
+                h0 = 4 * (groups[0] - 1)
+                heads = g_rest[b][:].rearrange("p (h i d) -> p h i d", h=7, i=PACK)[:, h0 : h0 + nh]
+            if part == 0:
+                products[u] = ring.tile([P, 2048], F32, name="products", bufs=2)
+            for k, i in enumerate(slots):
+                lo, hi = 0, nh
+                if k == len(slots) - 1:
+                    lo, hi = (0, nh - 1) if part == 0 else (nh - 1, nh)
+                elif part == 1:
+                    continue
+                n = hi - lo
+                nc.vector.tensor_tensor(
+                    out=products[u][:, k * 1024 : k * 1024 + 2 * nh * HD].rearrange("p (s h d) -> p s h d", s=2, h=nh)[:, :, lo:hi, :],
+                    in0=heads[:, lo:hi, i, :].unsqueeze(1).to_broadcast([P, 2, n, HD]),
+                    in1=table[:, i * P : (i + 1) * P].rearrange("p (s j) -> p s j", s=2).unsqueeze(2).to_broadcast([P, 2, 2 * n, HALF]),
+                    op=ALU.mult,
+                )
+
+        def rotate(u, engine):
+            b, slots, groups = UNITS[u]
+            nh = rotated_heads(groups)
+            n = len(slots)
+            width = 2048 // n
+            both = products[u][:].rearrange("p (k c) -> p k c", k=n)[:, :, 0 : 2 * nh * HD]
+            both = both.rearrange("p k (s h f j) -> p k s h f j", s=2, h=nh, f=2)
+            dz = dz_rows(b, groups)[:, slots[0] : slots[0] + n, 0 : nh * HD].rearrange("p k (h f j) -> p k h f j", h=nh, f=2)
+            engine.tensor_tensor(out=dz[:, :, :, 0, :], in0=both[:, :, 0, :, 0, :], in1=both[:, :, 1, :, 1, :], op=ALU.add)
+            engine.tensor_tensor(out=dz[:, :, :, 1, :], in0=both[:, :, 0, :, 1, :], in1=both[:, :, 1, :, 0, :], op=ALU.subtract)
+
+        def transpose_pair(first, second):
+            k, bank = take_bank()
+            for n, rows in enumerate((first, second)):
+                words = rows.bitcast(F32)
+                for u in range(2):
+                    nc.tensor.transpose(bank[:, (2 * n + u) * P : (2 * n + u + 1) * P], words[:, u::2], ident[:])
+            return k, bank
+
+        def empty_pair(k, bank, engine):
+            grouped = ring.tile([P, 2 * NW], BF16, name="grouped", align_bytes=64, bufs=12)
+            copy_on(
+                engine,
+                grouped[:].bitcast(F32).rearrange("p (n r u) -> p n r u", n=2, u=2),
+                bank[:].rearrange("p (n u r) -> p n r u", n=2, u=2),
+            )
+            free_banks.append(k)
+            return grouped
+
+        def pieces(u):
+            b, slots, groups = UNITS[u]
+            return [(b, i, g) for i in slots for g in groups]
+
+        def turn_dz(u):
+            first, second = [dz_rows(b, (g,))[:, i, :] for b, i, g in pieces(u)]
+            turned[u] = transpose_pair(first, second)
+
+        def empty_dz(u, engine):
+            turned[u] = empty_pair(turned[u][0], turned[u][1], engine)
+
+        def quantize_features(u):
+            codes = keep.tile([P, 2 * P], U32, name="zf_codes%d" % u, align_bytes=64)
+            scales = keep.tile([P, 2 * P], U8, name="zf_scales%d" % u, align_bytes=64)
+            nc.vector.quantize_mx(out=codes[:].bitcast(E5M2), scales=scales[:], in_=turned[u][:])
+            for n, piece in enumerate(pieces(u)):
+                zf_codes[piece] = codes[:, n * P : (n + 1) * P]
+                zf_scales[piece] = scales[:, n * P : (n + 1) * P]
+
+        def interleave(grouped, rows, engine):
+            copy_on(
+                engine,
+                grouped.rearrange("p (c n i) -> p c i n", n=4, i=PACK),
+                rows.rearrange("p i (c n) -> p c i n", n=4),
+            )
+
+        grouped_of, w_turned = {}, {}
+        for b in range(B):
+            for g in range(GROUPS):
+                zt_codes[b, g] = keep.tile([P, NW], U32, name="zt_codes%d_%d" % (b, g), align_bytes=64)
+                zt_scales[b, g] = keep.tile([P, NW], U8, name="zt_scales%d_%d" % (b, g), align_bytes=64)
+
+        def group(item, engine, gated=False):
+            kind, b, c, half = item
+            grouped_of[item] = ring.tile(
+                [P, PACK * X_PIECE], BF16, name="token_grouped", tag="gated" if gated else "free", align_bytes=64, bufs=1 if gated else 6
+            )
+            if kind == "x":
+                lo = c * X_PIECE
+                load = lo // NW
+                rows = x_raw[b, load][:, :, lo - load * NW : lo - load * NW + X_PIECE]
+            else:
+                rows = dz_rows(b, (c,))[:, :, half * X_PIECE : (half + 1) * X_PIECE]
+            interleave(grouped_of[item][:], rows, engine)
+
+        def quantize_grouped(item):
+            kind, b, c, half = item
+            if kind == "x":
+                cols = slice(c * X_PIECE, (c + 1) * X_PIECE)
+                nc.vector.quantize_mx(out=x_codes[b][:, cols].bitcast(E4M3), scales=x_scales[b][:, cols], in_=grouped_of[item][:])
+            else:
+                cols = slice(half * X_PIECE, (half + 1) * X_PIECE)
+                nc.vector.quantize_mx(out=zt_codes[b, c][:, cols].bitcast(E5M2), scales=zt_scales[b, c][:, cols], in_=grouped_of[item][:])
+            quantized.add(item)
+
+        def turn_w(pair, g):
+            cols = slice(g * NW, (g + 1) * NW)
+            w_turned[pair, g] = transpose_pair(w_raw[2 * pair][:, cols], w_raw[2 * pair + 1][:, cols])
+
+        def empty_w(pair, g):
+            w_turned[pair, g] = empty_pair(w_turned[pair, g][0], w_turned[pair, g][1], "scalar")
+
+        def quantize_w(pair, g):
+            cols = slice(pair * 2 * P, (pair + 1) * 2 * P)
+            nc.vector.quantize_mx(out=w_codes[g][:, cols].bitcast(E4M3), scales=w_scales[g][:, cols], in_=w_turned[pair, g][:])
+
+        opened = {}
+
+        def passes_of(job):
+            kind, a, c = job
+            if kind == "dx":
+                b, i = a
+                cols = slice(OUT0_WINDOWS[c][0], OUT0_WINDOWS[c][0] + NW)
+                return [
+                    (zf_codes.get((b, i, g)), zf_scales.get((b, i, g)), E5M2, w_codes[g][:, cols], w_scales[g][:, cols], E4M3)
+                    for g in range(GROUPS)
+                ]
+            cols = slice(a * P, (a + 1) * P)
+            return [
+                (x_codes[b][:, cols], x_scales[b][:, cols], E4M3, zt_codes.get((b, c)), zt_scales.get((b, c)), E5M2)
+                for b in range(B)
+            ]
+
+        def matmuls(job, stop_before=None):
+            steps = passes_of(job)
+            if job not in opened:
+                opened[job] = take_bank() + (0,)
+            k, bank, done = opened[job]
+            end = len(steps) if stop_before is None else stop_before
+            for n in range(done, end):
+                lhs, lhs_scale, lhs_type, rhs, rhs_scale, rhs_type = steps[n]
+                nc.tensor.matmul_mx(
+                    out=bank[:],
+                    lhsT=lhs[:].bitcast(lhs_type),
+                    lhsT_scale=lhs_scale[:],
+                    rhs=rhs[:].bitcast(rhs_type),
+                    rhs_scale=rhs_scale[:],
+                    start=(n == 0),
+                    stop=(n == len(steps) - 1),
+                )
+            opened[job] = (k, bank, end)
+
+        def store(job, engine):
+            kind, a, c = job
+            k, bank, done = opened[job]
+            if kind == "dx":
+                b, i = a
+                first, kept = OUT0_WINDOWS[c]
+                width = first + NW - kept
+                dest = out_0[b].rearrange("(p i) e -> p i e", i=PACK)[:, i, kept : kept + width]
+            else:
+                width = NW
+                dest = out_1[a * P : (a + 1) * P, c * NW : (c + 1) * NW]
+            result = keep.tile([P, width], F32, name="result", tag="w_or_out", bufs=E_TILES)
+            copy_on(engine, result[:], bank[:, NW - width :])
+            free_banks.append(k)
+            nc.sync.dma_start(out=dest, in_=result[:])
+
+        x_todo = [("x", b, c, 0) for c in range(E // X_PIECE) for b in range(B)]
+        w_todo = list(W_ORDER)
+        quantized, w_done, seen = set(), set(), set()
+        jobs, token_done = [], {}
+        for u in range(len(UNITS)):
+            seen.update(pieces(u))
+            token_done[u] = []
+            for b, i, g in pieces(u):
+                if all((b, n, g) in seen for n in range(PACK)) and (b, g) not in token_done[u]:
+                    token_done[u].append((b, g))
+                job = ("dx", (b, i), 0)
+                if all((b, i, n) in seen for n in range(GROUPS)) and job not in jobs:
+                    jobs.extend(("dx", (b, i), c) for c in range(3))
+            for b, g in token_done[u]:
+                if all((1 - b, n, g) in seen for n in range(PACK)):
+                    jobs.extend(("dw", e, g) for e in range(E_TILES))
+
+        def available(job):
+            kind, a, c = job
+            if kind == "dx":
+                first = OUT0_WINDOWS[c][0] // (2 * P)
+                have = [(a[0], a[1], g) in zf_codes and (first, g) in w_done and (first + 1, g) in w_done for g in range(GROUPS)]
+            else:
+                have = [("z", b, c, 0) in quantized and ("z", b, c, 1) in quantized and ("x", b, a * P // X_PIECE, 0) in quantized for b in range(B)]
+            return (have + [False]).index(False), len(have)
+
+        def run_jobs(budget, fillers, tail, hold=False):
+            n = 0
+            for job in list(jobs):
+                have, need = available(job)
+                done = opened[job][2] if job in opened else 0
+                if have == need and budget >= need - done and (job in opened or free_banks):
+                    matmuls(job)
+                    budget = budget - (need - done)
+                    jobs.remove(job)
+                    if hold and not held:
+                        held.append(job)
+                    else:
+                        store(job, "vector" if tail and n % TAIL_V == 0 else "scalar")
+                    n = n + 1
+                    if fillers and n % FILL_EVERY == 0:
+                        fillers.pop(0)()
+            for job in jobs[:AHEAD]:
+                have, need = available(job)
+                done = opened[job][2] if job in opened else 0
+                if done < have < need and budget >= have - done and (job in opened or len(free_banks) > RESERVE):
+                    matmuls(job, have)
+                    budget = budget - (have - done)
+            while fillers:
+                fillers.pop(0)()
+
+        nc.vector.memset(warm[:], 0.0)
+        nc.scalar.activation(out=warm[:], in_=warm[:], func=ACT.Sin)
+        w_now, z_todo, held, w_held = [], [], [], []
+        group(x_todo[0], "scalar")
+        build_table()
+        group(x_todo[1], "gpsimd")
+        group(x_todo[2], "scalar")
+        group(x_todo[3], "scalar")
+        s_due, s_next, x_todo = x_todo[0:2], x_todo[2:4], x_todo[4:]
+        last = len(UNITS)
+        for u in range(last):
+            multiply(u, 0)
+            if w_held:
+                item = w_held.pop()
+                w_turned[item] = empty_pair(w_turned[item][0], w_turned[item][1], "vector")
+                w_now.append(item)
+            elif held:
+                store(held.pop(), "vector")
+            hurried = []
+            if u > 0:
+                turn_dz(u - 1)
+                for b, g in reversed(token_done[u - 1]):
+                    (hurried if b == 1 else z_todo).extend(("z", b, g, half) for half in range(2))
+                if hurried:
+                    group(hurried[1], "scalar")
+                    group(hurried[0], "vector")
+                empty_dz(u - 1, "scalar")
+            if u < last - 1:
+                for item in s_due:
+                    quantize_grouped(item)
+            if u > 1:
+                quantize_features(u - 2)
+            for item in hurried:
+                quantize_grouped(item)
+            for n in range(min(QW_STEP[u], len(w_now))):
+                quantize_w(*w_now[0])
+                w_done.add(w_now.pop(0))
+            multiply(u, 1)
+            if u == last - 1:
+                quantize_grouped(s_due.pop())
+            rotate(u, nc.gpsimd if u < G_UNITS else nc.vector)
+            if u < last - 1:
+                s_due, s_next = s_next, []
+            for n in range(S_STEP[u]):
+                if x_todo or z_todo:
+                    s_next.append(z_todo.pop(0) if z_todo else x_todo.pop(0))
+            fillers = [lambda item=item: group(item, "scalar") for item in s_next]
+            for n in range(min(W_STEP[u], len(w_todo))):
+                item = w_todo.pop(0)
+                turn_w(*item)
+                if n == 0:
+                    w_held.append(item)
+                else:
+                    empty_w(*item)
+                    w_now.append(item)
+                if fillers:
+                    fillers.pop(0)()
+            run_jobs(BUDGET[u], fillers, False, not w_held)
+        while held:
+            store(held.pop(), "scalar")
+        urgent = [("z", b, g, half) for b, g in token_done[last - 1] for half in range(2)]
+        turn_dz(last - 1)
+        group(urgent[1], "scalar")
+        quantize_grouped(s_due.pop())
+        group(urgent[0], "vector")
+        empty_dz(last - 1, "scalar")
+        quantize_features(last - 2)
+        free_banks.append(0)
+        for item in urgent:
+            quantize_grouped(item)
+        run_jobs(TAIL_A, [], False)
+        quantize_features(last - 1)
+        jobs[:] = sorted(jobs, key=lambda job: job[0] == "dx" and job[1][1] >= 2)
+        run_jobs(999, [], True)
+        assert not jobs and not x_todo and not z_todo

@@ -6,6 +6,7 @@ from concourse.masks import make_identity
 
 B, T, E, H, HD = 2, 512, 1280, 10, 128
 J = (H + 2) * HD
+ROPE_BASE = 10000.0
 FLOPS = 2 * 2 * B * T * E * J
 
 F32 = mybir.dt.float32
@@ -19,33 +20,35 @@ ALU = mybir.AluOpType
 ACT = mybir.ActivationFunctionType
 
 P = 128
-PACK = 4
+SLOTS = 4
 HALF = HD // 2
-NW = 512
-GROUPS = J // NW
+BANK = 512
+BANKS = 8
+GROUPS = J // BANK
+GROUP_HEADS = BANK // HD
+LATER_HEADS = H + 1 - GROUP_HEADS
 E_TILES = E // P
-X_PIECE = 256
-X_LOADS = ((0, 512), (512, 1024), (1024, 1280))
-OUT0_WINDOWS = ((0, 0), (512, 512), (768, 1024))
-ROUND = 1.5 * 2.0**23
-UNITS = (
+W_PAIRS = E_TILES // 2
+PIECE = 256
+X_LOADS = ((0, 512), (512, 1024), (1024, E))
+WINDOWS = ((0, 0), (512, 512), (E - BANK, 1024))
+ROUNDING = 1.5 * 2.0**23
+
+STEPS = (
     [(b, (i, i + 1), (0,)) for b in range(B) for i in (0, 2)]
-    + [(0, (i,), (1, 2)) for i in range(PACK)]
+    + [(0, (i,), (1, 2)) for i in range(SLOTS)]
     + [(1, (i,), (1, 2)) for i in (0, 1)]
     + [(1, (2, 3), (g,)) for g in (2, 1)]
 )
-G_UNITS = 11
-LOADS = "X00 F0 X10 W0 W1 X01 W2 W3 X11 F1 W4 W5 X02 X12 W6 W7 R0 W8 W9 R1"
-W_ORDER = [(p, g) for p in range(5) for g in range(3)]
-W_STEP = (3, 3, 3, 3, 3, 0, 0, 0, 0, 0, 0, 0, 0)
-S_STEP = (2, 2, 2, 2, 0, 0, 0, 0, 2, 2, 0, 0, 0)
-QW_STEP = (0, 2, 2, 2, 2, 3, 3, 3, 0, 0, 0, 0)
-BUDGET = (0, 0, 0, 2, 6, 12, 12, 12, 12, 12, 12, 12)
-AHEAD = 5
-RESERVE = 2
-TAIL_V = 2
-FILL_EVERY = 2
-TAIL_A = 12
+FIRST_ROW_STEP = 2 * B
+LAST = len(STEPS) - 1
+
+W_BANKS_PER_STEP = 3
+COPIES_PER_STEP = 2
+PASSES_PER_STEP = 12
+OPEN_AHEAD = 5
+SPARE_BANKS = 2
+VECTOR_HEADS = 2
 
 
 def tile_multiqueryattention_pa_v_kernel(tc, x, w_attn, grad_0, grad_1, grad_2, out_0, out_1):
@@ -53,431 +56,459 @@ def tile_multiqueryattention_pa_v_kernel(tc, x, w_attn, grad_0, grad_1, grad_2, 
 
     with ExitStack() as ctx:
         keep = ctx.enter_context(tc.tile_pool(name="keep", bufs=1))
-        ring = ctx.enter_context(tc.tile_pool(name="ring", bufs=3))
+        ring = ctx.enter_context(tc.tile_pool(name="ring", bufs=2))
         psum = ctx.enter_context(tc.psum_pool(name="psum", bufs=1))
         ctx.enter_context(tc.manual_schedule())
 
-        free_banks = list(range(1, 8))
+        free_banks = list(range(1, BANKS))
 
         def take_bank():
-            k = free_banks.pop(0)
-            return k, psum.tile([P, NW], F32, name="bank", tag="bank%d" % k)
+            number = free_banks.pop(0)
+            return number, psum.tile([P, BANK], F32, name="bank", tag="bank%d" % number)
 
-        g_first, g_rest, dz_first, dz_rest, x_raw, w_raw = {}, {}, {}, {}, {}, {}
+        grad_first, grad_later, x_rows, w_rows = {}, {}, {}, {}
+        dz_first = [keep.tile([P, SLOTS * BANK], BF16, name="dz_first%d" % b, align_bytes=64) for b in range(B)]
+        dz_later = [keep.tile([P, SLOTS * 2 * BANK], BF16, name="dz_later%d" % b, align_bytes=64) for b in range(B)]
 
-        def load_first(b):
-            g_first[b] = keep.tile([P, 4 * T], BF16, name="g_first%d" % b)
+        def load_first_group(b):
+            grad_first[b] = keep.tile([P, GROUP_HEADS * T], BF16, name="grad_first%d" % b)
             nc.sync.dma_start(
-                out=g_first[b][:].rearrange("p (h c) -> p h c", h=4),
-                in_=grad_0[b, 0:4].rearrange("h (p i) d -> p h (i d)", i=PACK),
+                out=grad_first[b][:].rearrange("p (h c) -> p h c", h=GROUP_HEADS),
+                in_=grad_0[b, 0:GROUP_HEADS].rearrange("h (p i) d -> p h (i d)", i=SLOTS),
             )
 
-        def load_rest(b):
-            g_rest[b] = keep.tile([P, 7 * T], BF16, name="g_rest%d" % b)
+        def load_later_groups(b):
+            query_heads = H - GROUP_HEADS
+            grad_later[b] = keep.tile([P, LATER_HEADS * T], BF16, name="grad_later%d" % b)
             nc.sync.dma_start(
-                out=g_rest[b][:, 0 : 6 * T].rearrange("p (h c) -> p h c", h=6),
-                in_=grad_0[b, 4:H].rearrange("h (p i) d -> p h (i d)", i=PACK),
+                out=grad_later[b][:, 0 : query_heads * T].rearrange("p (h c) -> p h c", h=query_heads),
+                in_=grad_0[b, GROUP_HEADS:H].rearrange("h (p i) d -> p h (i d)", i=SLOTS),
             )
-            nc.sync.dma_start(out=g_rest[b][:, 6 * T :], in_=grad_1[b, 0].rearrange("(p i) d -> p (i d)", i=PACK))
             nc.sync.dma_start(
-                out=dz_rest[b][:].rearrange("p (i c) -> p i c", i=PACK)[:, :, 7 * HD :],
-                in_=grad_2[b, 0].rearrange("(p i) d -> p i d", i=PACK),
+                out=grad_later[b][:, query_heads * T :], in_=grad_1[b, 0].rearrange("(p i) d -> p (i d)", i=SLOTS)
+            )
+            nc.sync.dma_start(
+                out=dz_later[b][:].rearrange("p (i c) -> p i c", i=SLOTS)[:, :, LATER_HEADS * HD :],
+                in_=grad_2[b, 0].rearrange("(p i) d -> p i d", i=SLOTS),
             )
 
-        def load_x(b, c):
-            lo, hi = X_LOADS[c]
-            x_raw[b, c] = keep.tile([P, PACK, hi - lo], BF16, name="x_raw%d_%d" % (b, c))
-            nc.sync.dma_start(out=x_raw[b, c][:], in_=x[b].rearrange("(p i) e -> p i e", i=PACK)[:, :, lo:hi])
+        def load_x(b, part):
+            lo, hi = X_LOADS[part]
+            x_rows[b, part] = keep.tile([P, SLOTS, hi - lo], BF16, name="x_rows%d_%d" % (b, part))
+            nc.sync.dma_start(out=x_rows[b, part][:], in_=x[b].rearrange("(p i) e -> p i e", i=SLOTS)[:, :, lo:hi])
 
-        def load_w(r):
-            w_raw[r] = keep.tile([P, J], BF16, name="w_raw", tag="w_or_out", bufs=E_TILES)
-            nc.sync.dma_start(out=w_raw[r][:], in_=w_attn[r * P : (r + 1) * P, :])
+        def load_w(pair):
+            for r in (2 * pair, 2 * pair + 1):
+                w_rows[r] = keep.tile([P, J], BF16, name="w_rows", tag="w_then_results", bufs=E_TILES)
+                nc.sync.dma_start(out=w_rows[r][:], in_=w_attn[r * P : (r + 1) * P, :])
 
-        for b in range(B):
-            dz_first[b] = keep.tile([P, PACK * NW], BF16, name="dz_first%d" % b, align_bytes=64)
-            dz_rest[b] = keep.tile([P, PACK * 2 * NW], BF16, name="dz_rest%d" % b, align_bytes=64)
-
-        for word in LOADS.split():
-            if word[0] == "F":
-                load_first(int(word[1]))
-            elif word[0] == "R":
-                load_rest(int(word[1]))
-            elif word[0] == "W":
-                load_w(int(word[1]))
-            else:
-                load_x(int(word[1]), int(word[2]))
+        load_w(0)
+        load_first_group(0)
+        load_x(0, 0)
+        load_w(1)
+        load_x(1, 0)
+        load_w(2)
+        load_first_group(1)
+        load_x(0, 1)
+        load_x(1, 1)
+        load_w(3)
+        load_w(4)
+        load_later_groups(0)
+        load_x(0, 2)
+        load_x(1, 2)
+        load_later_groups(1)
 
         ident = keep.tile([P, P], F32, name="ident")
-        pos = keep.tile([P, T], F32, name="pos")
+        positions = keep.tile([P, T], F32, name="positions")
         make_identity(nc, ident[:])
-        nc.gpsimd.iota(pos[:], pattern=[[1, PACK], [PACK, P]], base=0, channel_multiplier=0, allow_small_or_imprecise_dtypes=True)
+        nc.gpsimd.iota(
+            positions[:],
+            pattern=[[1, SLOTS], [SLOTS, P]],
+            base=0,
+            channel_multiplier=0,
+            allow_small_or_imprecise_dtypes=True,
+        )
+        table = psum.tile([P, BANK], F32, name="table", tag="bank0")
 
-        table = psum.tile([P, NW], F32, name="table", tag="bank0")
+        phase = keep.tile([P, 1], F32, name="phase")
+        nc.vector.memset(phase[0:HALF, :], 0.25)
+        nc.vector.memset(phase[HALF:P, :], 0.0)
+        nc.scalar.activation(out=phase[HALF:P, :], in_=phase[HALF:P, :], func=ACT.Sin)
 
         def build_table():
+            split = 8
             one = keep.tile([P, 1], F32, name="one")
-            phase = keep.tile([P, 1], F32, name="phase")
-            factors = keep.tile([P, 16], F32, name="factors")
-            freqs = keep.tile([P, HALF], F32, name="freqs")
-            picked = keep.tile([P, P], F32, name="picked")
+            factors = keep.tile([P, 2 * split], F32, name="factors")
+            all_freqs = keep.tile([P, HALF], F32, name="all_freqs")
+            masked = keep.tile([P, P], F32, name="masked")
             freq = keep.tile([P, 1], F32, name="freq")
             nc.vector.memset(one[:], 1.0)
-            nc.vector.memset(phase[0:HALF, :], 0.25)
-            nc.vector.memset(phase[HALF:P, :], 0.0)
-            for a in range(8):
-                coarse = 10000.0 ** (-32.0 * a / HD)
-                fine = 10000.0 ** (-(4.0 * a + 1.0) / HD) / (2.0 * math.pi)
+            for a in range(split):
+                coarse = ROPE_BASE ** (-4.0 * split * a / HD)
+                fine = ROPE_BASE ** (-(4.0 * a + 1.0) / HD) / (2.0 * math.pi)
                 nc.vector.tensor_scalar(factors[:, a : a + 1], one[:], coarse, None, ALU.mult)
-                nc.vector.tensor_scalar(factors[:, 8 + a : 9 + a], one[:], fine, None, ALU.mult)
+                nc.vector.tensor_scalar(factors[:, split + a : split + a + 1], one[:], fine, None, ALU.mult)
             nc.vector.tensor_tensor(
-                out=freqs[:].rearrange("p (a c) -> p a c", a=8),
-                in0=factors[:, 0:8].unsqueeze(2).to_broadcast([P, 8, 8]),
-                in1=factors[:, 8:16].unsqueeze(1).to_broadcast([P, 8, 8]),
+                out=all_freqs[:].rearrange("p (a c) -> p a c", a=split),
+                in0=factors[:, 0:split].unsqueeze(2).to_broadcast([P, split, split]),
+                in1=factors[:, split:].unsqueeze(1).to_broadcast([P, split, split]),
                 op=ALU.mult,
             )
             nc.vector.scalar_tensor_tensor(
-                out=picked[:].rearrange("p (s j) -> p s j", s=2),
+                out=masked[:].rearrange("p (s j) -> p s j", s=2),
                 in0=ident[:].rearrange("p (s j) -> p s j", s=2),
                 scalar=1.0,
-                in1=freqs[:].unsqueeze(1).to_broadcast([P, 2, HALF]),
+                in1=all_freqs[:].unsqueeze(1).to_broadcast([P, 2, HALF]),
                 op0=ALU.mult,
                 op1=ALU.mult,
                 accum_out=freq[:],
             )
-            halves = [slice(0, T // 2), slice(T // 2, T)]
+            halves = (slice(0, T // 2), slice(T // 2, T))
             turns = keep.tile([P, T], F32, name="turns")
             whole = keep.tile([P, T], I32, name="whole")
-            rest = keep.tile([P, T], F32, name="rest")
+            minus_rest = keep.tile([P, T], F32, name="minus_rest")
             for s in halves:
-                nc.vector.tensor_scalar(turns[:, s], pos[:, s], freq[:], phase[:], ALU.mult, ALU.add)
+                nc.vector.tensor_scalar(turns[:, s], positions[:, s], freq[:], phase[:], ALU.mult, ALU.add)
             for s in halves:
-                nc.vector.tensor_scalar(whole[:, s], turns[:, s], ROUND, None, ALU.add)
+                nc.vector.tensor_scalar(whole[:, s], turns[:, s], ROUNDING, None, ALU.add)
             for s in halves:
-                nc.vector.scalar_tensor_tensor(rest[:, s], whole[:, s], ROUND, turns[:, s], ALU.subtract, ALU.subtract)
+                nc.vector.scalar_tensor_tensor(
+                    minus_rest[:, s], whole[:, s], ROUNDING, turns[:, s], ALU.subtract, ALU.subtract
+                )
+            waves = keep.tile([P, T], F32, name="waves")
             for s in halves:
-                nc.scalar.activation(out=pos[:, s], in_=rest[:, s], func=ACT.Sin, scale=-2.0 * math.pi)
-            for i in range(PACK):
-                nc.tensor.transpose(table[:, i * P : (i + 1) * P], pos[:, i * P : (i + 1) * P], ident[:])
+                nc.scalar.activation(out=waves[:, s], in_=minus_rest[:, s], func=ACT.Sin, scale=-2.0 * math.pi)
+            for i in range(SLOTS):
+                nc.tensor.transpose(table[:, i * P : (i + 1) * P], waves[:, i * P : (i + 1) * P], ident[:])
 
-        warm = keep.tile([P, 1], F32, name="warm")
+        products = {}
 
-        products, turned, zf_codes, zf_scales, zt_codes, zt_scales = {}, {}, {}, {}, {}, {}
-        x_codes = [keep.tile([P, E], U32, name="x_codes%d" % b, align_bytes=64) for b in range(B)]
-        x_scales = [keep.tile([P, E], U8, name="x_scales%d" % b, align_bytes=64) for b in range(B)]
-        w_codes = [keep.tile([P, E], U32, name="w_codes%d" % g, align_bytes=64) for g in range(GROUPS)]
-        w_scales = [keep.tile([P, E], U8, name="w_scales%d" % g, align_bytes=64) for g in range(GROUPS)]
+        def dz_slots(b, groups):
+            if groups[0] == 0:
+                return dz_first[b][:].rearrange("p (i c) -> p i c", i=SLOTS)
+            lo = (groups[0] - 1) * BANK
+            return dz_later[b][:].rearrange("p (i c) -> p i c", i=SLOTS)[:, :, lo : lo + BANK * len(groups)]
+
+        def rotated_heads(groups):
+            return sum(GROUP_HEADS - 1 if g == GROUPS - 1 else GROUP_HEADS for g in groups)
+
+        def multiply(step, last_head):
+            b, slots, groups = STEPS[step]
+            count = rotated_heads(groups)
+            if groups[0] == 0:
+                heads = grad_first[b][:].rearrange("p (h i d) -> p h i d", h=GROUP_HEADS, i=SLOTS)
+            else:
+                first = GROUP_HEADS * (groups[0] - 1)
+                heads = grad_later[b][:].rearrange("p (h i d) -> p h i d", h=LATER_HEADS, i=SLOTS)[:, first : first + count]
+            if last_head:
+                parts = [(len(slots) - 1, count - 1, count)]
+            else:
+                products[step] = ring.tile([P, 4 * BANK], F32, name="products")
+                parts = [(n, 0, count) for n in range(len(slots) - 1)] + [(len(slots) - 1, 0, count - 1)]
+            for n, lo, hi in parts:
+                i = slots[n]
+                out = products[step][:, n * 2 * BANK : n * 2 * BANK + 2 * count * HD]
+                waves = table[:, i * P : (i + 1) * P].rearrange("p (s j) -> p s j", s=2)
+                nc.vector.tensor_tensor(
+                    out=out.rearrange("p (s h d) -> p s h d", s=2, h=count)[:, :, lo:hi, :],
+                    in0=heads[:, lo:hi, i, :].unsqueeze(1).to_broadcast([P, 2, hi - lo, HD]),
+                    in1=waves.unsqueeze(2).to_broadcast([P, 2, 2 * (hi - lo), HALF]),
+                    op=ALU.mult,
+                )
+
+        def rotation_views(step):
+            b, slots, groups = STEPS[step]
+            count = rotated_heads(groups)
+            both = products[step][:].rearrange("p (n c) -> p n c", n=len(slots))[:, :, 0 : 2 * count * HD]
+            both = both.rearrange("p n (s h f j) -> p n s h f j", s=2, h=count, f=2)
+            dz = dz_slots(b, groups)[:, slots[0] : slots[0] + len(slots), 0 : count * HD]
+            return both[:, :, 0], both[:, :, 1], dz.rearrange("p n (h f j) -> p n h f j", h=count, f=2)
+
+        def lower_half(step, engine):
+            by_cos, by_sin, dz = rotation_views(step)
+            engine.tensor_tensor(out=dz[:, :, :, 0, :], in0=by_cos[:, :, :, 0, :], in1=by_sin[:, :, :, 1, :], op=ALU.add)
+
+        def upper_half(step, engine, heads):
+            by_cos, by_sin, dz = rotation_views(step)
+            engine.tensor_tensor(
+                out=dz[:, :, heads, 1, :], in0=by_cos[:, :, heads, 1, :], in1=by_sin[:, :, heads, 0, :], op=ALU.subtract
+            )
+
+        def gpsimd_heads(step):
+            if 0 < step <= FIRST_ROW_STEP:
+                return rotated_heads(STEPS[step][2]) - VECTOR_HEADS // len(STEPS[step][1])
+            return 0
 
         def copy_on(engine, out, in_):
             if engine == "vector":
                 nc.vector.tensor_copy(out=out, in_=in_)
-            elif engine == "gpsimd":
-                nc.gpsimd.tensor_scalar(out, in_, 1.0, 0.0, ALU.mult, ALU.add)
-            else:
+            elif engine == "scalar":
                 nc.scalar.copy(out=out, in_=in_)
-
-        def dz_rows(b, groups):
-            if groups[0] == 0:
-                return dz_first[b][:].rearrange("p (i c) -> p i c", i=PACK)
-            lo = (groups[0] - 1) * NW
-            return dz_rest[b][:].rearrange("p (i c) -> p i c", i=PACK)[:, :, lo : lo + NW * len(groups)]
-
-        def rotated_heads(groups):
-            return sum(3 if g == GROUPS - 1 else 4 for g in groups)
-
-        def multiply(u, part):
-            b, slots, groups = UNITS[u]
-            nh = rotated_heads(groups)
-            if groups[0] == 0:
-                heads = g_first[b][:].rearrange("p (h i d) -> p h i d", h=4, i=PACK)
             else:
-                h0 = 4 * (groups[0] - 1)
-                heads = g_rest[b][:].rearrange("p (h i d) -> p h i d", h=7, i=PACK)[:, h0 : h0 + nh]
-            if part == 0:
-                products[u] = ring.tile([P, 2048], F32, name="products", bufs=2)
-            for k, i in enumerate(slots):
-                lo, hi = 0, nh
-                if k == len(slots) - 1:
-                    lo, hi = (0, nh - 1) if part == 0 else (nh - 1, nh)
-                elif part == 1:
-                    continue
-                n = hi - lo
-                nc.vector.tensor_tensor(
-                    out=products[u][:, k * 1024 : k * 1024 + 2 * nh * HD].rearrange("p (s h d) -> p s h d", s=2, h=nh)[:, :, lo:hi, :],
-                    in0=heads[:, lo:hi, i, :].unsqueeze(1).to_broadcast([P, 2, n, HD]),
-                    in1=table[:, i * P : (i + 1) * P].rearrange("p (s j) -> p s j", s=2).unsqueeze(2).to_broadcast([P, 2, 2 * n, HALF]),
-                    op=ALU.mult,
-                )
+                nc.gpsimd.tensor_scalar(out, in_, 1.0, 0.0, ALU.mult, ALU.add)
 
-        def rotate(u, engine):
-            b, slots, groups = UNITS[u]
-            nh = rotated_heads(groups)
-            n = len(slots)
-            width = 2048 // n
-            both = products[u][:].rearrange("p (k c) -> p k c", k=n)[:, :, 0 : 2 * nh * HD]
-            both = both.rearrange("p k (s h f j) -> p k s h f j", s=2, h=nh, f=2)
-            dz = dz_rows(b, groups)[:, slots[0] : slots[0] + n, 0 : nh * HD].rearrange("p k (h f j) -> p k h f j", h=nh, f=2)
-            engine.tensor_tensor(out=dz[:, :, :, 0, :], in0=both[:, :, 0, :, 0, :], in1=both[:, :, 1, :, 1, :], op=ALU.add)
-            engine.tensor_tensor(out=dz[:, :, :, 1, :], in0=both[:, :, 0, :, 1, :], in1=both[:, :, 1, :, 0, :], op=ALU.subtract)
-
-        def transpose_pair(first, second):
-            k, bank = take_bank()
+        def transpose_words(first, second):
+            number, bank = take_bank()
             for n, rows in enumerate((first, second)):
                 words = rows.bitcast(F32)
                 for u in range(2):
                     nc.tensor.transpose(bank[:, (2 * n + u) * P : (2 * n + u + 1) * P], words[:, u::2], ident[:])
-            return k, bank
+            return number, bank
 
-        def empty_pair(k, bank, engine):
-            grouped = ring.tile([P, 2 * NW], BF16, name="grouped", align_bytes=64, bufs=12)
+        def empty_words(filled, engine, name, bufs):
+            number, bank = filled
+            packed = ring.tile([P, 2 * BANK], BF16, name=name, align_bytes=64, bufs=bufs)
             copy_on(
                 engine,
-                grouped[:].bitcast(F32).rearrange("p (n r u) -> p n r u", n=2, u=2),
+                packed[:].bitcast(F32).rearrange("p (n r u) -> p n r u", n=2, u=2),
                 bank[:].rearrange("p (n u r) -> p n r u", n=2, u=2),
             )
-            free_banks.append(k)
-            return grouped
+            free_banks.append(number)
+            return packed
 
-        def pieces(u):
-            b, slots, groups = UNITS[u]
+        def mx_tiles(name, width):
+            codes = keep.tile([P, width], U32, name=name + "_codes", align_bytes=64)
+            scales = keep.tile([P, width], U8, name=name + "_scales", align_bytes=64)
+            return codes, scales
+
+        def quantize(target, columns, dtype, packed):
+            codes, scales = target
+            nc.vector.quantize_mx(out=codes[:, columns].bitcast(dtype), scales=scales[:, columns], in_=packed[:])
+
+        x_mx = [mx_tiles("x%d" % b, E) for b in range(B)]
+        w_mx = [mx_tiles("w%d" % g, E) for g in range(GROUPS)]
+        dz_token_mx = {(b, g): mx_tiles("dz_token%d_%d" % (b, g), BANK) for b in range(B) for g in range(GROUPS)}
+        dz_feature_mx = {}
+        quantized = set()
+        dz_banks, dz_packed, w_packed, piece_packed = {}, {}, {}, {}
+
+        def blocks(step):
+            b, slots, groups = STEPS[step]
             return [(b, i, g) for i in slots for g in groups]
 
-        def turn_dz(u):
-            first, second = [dz_rows(b, (g,))[:, i, :] for b, i, g in pieces(u)]
-            turned[u] = transpose_pair(first, second)
+        def turn_dz(step):
+            first, second = [dz_slots(b, (g,))[:, i, :] for b, i, g in blocks(step)]
+            dz_banks[step] = transpose_words(first, second)
 
-        def empty_dz(u, engine):
-            turned[u] = empty_pair(turned[u][0], turned[u][1], engine)
+        def empty_dz(step, engine):
+            dz_packed[step] = empty_words(dz_banks[step], engine, "dz_packed", 3)
 
-        def quantize_features(u):
-            codes = keep.tile([P, 2 * P], U32, name="zf_codes%d" % u, align_bytes=64)
-            scales = keep.tile([P, 2 * P], U8, name="zf_scales%d" % u, align_bytes=64)
-            nc.vector.quantize_mx(out=codes[:].bitcast(E5M2), scales=scales[:], in_=turned[u][:])
-            for n, piece in enumerate(pieces(u)):
-                zf_codes[piece] = codes[:, n * P : (n + 1) * P]
-                zf_scales[piece] = scales[:, n * P : (n + 1) * P]
+        def quantize_features(step):
+            codes, scales = mx_tiles("dz_feature%d" % step, 2 * P)
+            quantize((codes, scales), slice(0, 2 * P), E5M2, dz_packed[step])
+            for n, block in enumerate(blocks(step)):
+                dz_feature_mx[block] = (codes[:, n * P : (n + 1) * P], scales[:, n * P : (n + 1) * P])
 
-        def interleave(grouped, rows, engine):
+        def turn_w(pair, g):
+            columns = slice(g * BANK, (g + 1) * BANK)
+            return transpose_words(w_rows[2 * pair][:, columns], w_rows[2 * pair + 1][:, columns])
+
+        def empty_w(pair, g, filled):
+            w_packed[pair, g] = empty_words(filled, "scalar", "w_packed", 11)
+
+        def interleave(piece, engine):
+            if piece[0] == "x":
+                part, lo = divmod(piece[2] * PIECE, BANK)
+                rows = x_rows[piece[1], part][:, :, lo : lo + PIECE]
+            else:
+                rows = dz_slots(piece[1], (piece[2],))[:, :, piece[3] * PIECE : (piece[3] + 1) * PIECE]
+            piece_packed[piece] = ring.tile([P, SLOTS * PIECE], BF16, name="piece_packed", align_bytes=64, bufs=9)
             copy_on(
                 engine,
-                grouped.rearrange("p (c n i) -> p c i n", n=4, i=PACK),
+                piece_packed[piece][:].rearrange("p (c n i) -> p c i n", n=4, i=SLOTS),
                 rows.rearrange("p i (c n) -> p c i n", n=4),
             )
 
-        grouped_of, w_turned = {}, {}
-        for b in range(B):
-            for g in range(GROUPS):
-                zt_codes[b, g] = keep.tile([P, NW], U32, name="zt_codes%d_%d" % (b, g), align_bytes=64)
-                zt_scales[b, g] = keep.tile([P, NW], U8, name="zt_scales%d_%d" % (b, g), align_bytes=64)
-
-        def group(item, engine, gated=False):
-            kind, b, c, half = item
-            grouped_of[item] = ring.tile(
-                [P, PACK * X_PIECE], BF16, name="token_grouped", tag="gated" if gated else "free", align_bytes=64, bufs=1 if gated else 6
-            )
-            if kind == "x":
-                lo = c * X_PIECE
-                load = lo // NW
-                rows = x_raw[b, load][:, :, lo - load * NW : lo - load * NW + X_PIECE]
+        def quantize_piece(piece):
+            if piece[0] == "w":
+                pair, g = piece[1:]
+                quantize(w_mx[g], slice(pair * 2 * P, (pair + 1) * 2 * P), E4M3, w_packed[pair, g])
+            elif piece[0] == "x":
+                quantize(x_mx[piece[1]], slice(piece[2] * PIECE, (piece[2] + 1) * PIECE), E4M3, piece_packed[piece])
             else:
-                rows = dz_rows(b, (c,))[:, :, half * X_PIECE : (half + 1) * X_PIECE]
-            interleave(grouped_of[item][:], rows, engine)
+                target = dz_token_mx[piece[1], piece[2]]
+                quantize(target, slice(piece[3] * PIECE, (piece[3] + 1) * PIECE), E5M2, piece_packed[piece])
+            quantized.add(piece)
 
-        def quantize_grouped(item):
-            kind, b, c, half = item
-            if kind == "x":
-                cols = slice(c * X_PIECE, (c + 1) * X_PIECE)
-                nc.vector.quantize_mx(out=x_codes[b][:, cols].bitcast(E4M3), scales=x_scales[b][:, cols], in_=grouped_of[item][:])
-            else:
-                cols = slice(half * X_PIECE, (half + 1) * X_PIECE)
-                nc.vector.quantize_mx(out=zt_codes[b, c][:, cols].bitcast(E5M2), scales=zt_scales[b, c][:, cols], in_=grouped_of[item][:])
-            quantized.add(item)
+        def dz_halves(b, g):
+            return [("dz", b, g, half) for half in range(BANK // PIECE)]
 
-        def turn_w(pair, g):
-            cols = slice(g * NW, (g + 1) * NW)
-            w_turned[pair, g] = transpose_pair(w_raw[2 * pair][:, cols], w_raw[2 * pair + 1][:, cols])
-
-        def empty_w(pair, g):
-            w_turned[pair, g] = empty_pair(w_turned[pair, g][0], w_turned[pair, g][1], "scalar")
-
-        def quantize_w(pair, g):
-            cols = slice(pair * 2 * P, (pair + 1) * 2 * P)
-            nc.vector.quantize_mx(out=w_codes[g][:, cols].bitcast(E4M3), scales=w_scales[g][:, cols], in_=w_turned[pair, g][:])
+        def w_pieces(pairs):
+            return [("w", pair, g) for pair in pairs for g in range(GROUPS)]
 
         opened = {}
 
-        def passes_of(job):
-            kind, a, c = job
-            if kind == "dx":
-                b, i = a
-                cols = slice(OUT0_WINDOWS[c][0], OUT0_WINDOWS[c][0] + NW)
-                return [
-                    (zf_codes.get((b, i, g)), zf_scales.get((b, i, g)), E5M2, w_codes[g][:, cols], w_scales[g][:, cols], E4M3)
+        def passes_ready(tile):
+            if tile[0] == "dx":
+                pair = WINDOWS[tile[3]][0] // (2 * P)
+                ready = [
+                    (tile[1], tile[2], g) in dz_feature_mx and {("w", pair, g), ("w", pair + 1, g)} <= quantized
                     for g in range(GROUPS)
                 ]
-            cols = slice(a * P, (a + 1) * P)
-            return [
-                (x_codes[b][:, cols], x_scales[b][:, cols], E4M3, zt_codes.get((b, c)), zt_scales.get((b, c)), E5M2)
-                for b in range(B)
-            ]
+            else:
+                ready = [set(dz_halves(b, tile[2]) + [("x", b, tile[1] * P // PIECE)]) <= quantized for b in range(B)]
+            return (ready + [False]).index(False), len(ready)
 
-        def matmuls(job, stop_before=None):
-            steps = passes_of(job)
-            if job not in opened:
-                opened[job] = take_bank() + (0,)
-            k, bank, done = opened[job]
-            end = len(steps) if stop_before is None else stop_before
+        def matmuls(tile, end, total):
+            if tile not in opened:
+                opened[tile] = take_bank() + (0,)
+            number, bank, done = opened[tile]
             for n in range(done, end):
-                lhs, lhs_scale, lhs_type, rhs, rhs_scale, rhs_type = steps[n]
+                if tile[0] == "dx":
+                    columns = slice(WINDOWS[tile[3]][0], WINDOWS[tile[3]][0] + BANK)
+                    codes, scales = dz_feature_mx[tile[1], tile[2], n]
+                    lhs, lhs_scale = codes.bitcast(E5M2), scales
+                    rhs, rhs_scale = w_mx[n][0][:, columns].bitcast(E4M3), w_mx[n][1][:, columns]
+                else:
+                    columns = slice(tile[1] * P, (tile[1] + 1) * P)
+                    codes, scales = dz_token_mx[n, tile[2]]
+                    lhs, lhs_scale = x_mx[n][0][:, columns].bitcast(E4M3), x_mx[n][1][:, columns]
+                    rhs, rhs_scale = codes[:].bitcast(E5M2), scales[:]
                 nc.tensor.matmul_mx(
                     out=bank[:],
-                    lhsT=lhs[:].bitcast(lhs_type),
-                    lhsT_scale=lhs_scale[:],
-                    rhs=rhs[:].bitcast(rhs_type),
-                    rhs_scale=rhs_scale[:],
+                    lhsT=lhs,
+                    lhsT_scale=lhs_scale,
+                    rhs=rhs,
+                    rhs_scale=rhs_scale,
                     start=(n == 0),
-                    stop=(n == len(steps) - 1),
+                    stop=(n == total - 1),
                 )
-            opened[job] = (k, bank, end)
+            opened[tile] = (number, bank, end)
 
-        def store(job, engine):
-            kind, a, c = job
-            k, bank, done = opened[job]
-            if kind == "dx":
-                b, i = a
-                first, kept = OUT0_WINDOWS[c]
-                width = first + NW - kept
-                dest = out_0[b].rearrange("(p i) e -> p i e", i=PACK)[:, i, kept : kept + width]
+        def store(tile, engine):
+            number, bank = opened[tile][0:2]
+            if tile[0] == "dx":
+                first, kept = WINDOWS[tile[3]]
+                width = first + BANK - kept
+                dest = out_0[tile[1]].rearrange("(p i) e -> p i e", i=SLOTS)[:, tile[2], kept : kept + width]
             else:
-                width = NW
-                dest = out_1[a * P : (a + 1) * P, c * NW : (c + 1) * NW]
-            result = keep.tile([P, width], F32, name="result", tag="w_or_out", bufs=E_TILES)
-            copy_on(engine, result[:], bank[:, NW - width :])
-            free_banks.append(k)
+                width = BANK
+                dest = out_1[tile[1] * P : (tile[1] + 1) * P, tile[2] * BANK : (tile[2] + 1) * BANK]
+            result = keep.tile([P, width], F32, name="result", tag="w_then_results", bufs=E_TILES)
+            copy_on(engine, result[:], bank[:, BANK - width :])
+            free_banks.append(number)
             nc.sync.dma_start(out=dest, in_=result[:])
 
-        x_todo = [("x", b, c, 0) for c in range(E // X_PIECE) for b in range(B)]
-        w_todo = list(W_ORDER)
-        quantized, w_done, seen = set(), set(), set()
-        jobs, token_done = [], {}
-        for u in range(len(UNITS)):
-            seen.update(pieces(u))
-            token_done[u] = []
-            for b, i, g in pieces(u):
-                if all((b, n, g) in seen for n in range(PACK)) and (b, g) not in token_done[u]:
-                    token_done[u].append((b, g))
-                job = ("dx", (b, i), 0)
-                if all((b, i, n) in seen for n in range(GROUPS)) and job not in jobs:
-                    jobs.extend(("dx", (b, i), c) for c in range(3))
-            for b, g in token_done[u]:
-                if all((1 - b, n, g) in seen for n in range(PACK)):
-                    jobs.extend(("dw", e, g) for e in range(E_TILES))
+        tiles_left, groups_done, seen = [], {}, set()
+        for step in range(len(STEPS)):
+            seen.update(blocks(step))
+            b, slots, groups = STEPS[step]
+            groups_done[step] = [g for g in groups if {(b, i, g) for i in range(SLOTS)} <= seen]
+            for i in slots:
+                if {(b, i, g) for g in range(GROUPS)} <= seen:
+                    tiles_left.extend(("dx", b, i, window) for window in range(len(WINDOWS)))
+            if b == B - 1:
+                tiles_left.extend(("dw", r, g) for g in groups_done[step] for r in range(E_TILES))
 
-        def available(job):
-            kind, a, c = job
-            if kind == "dx":
-                first = OUT0_WINDOWS[c][0] // (2 * P)
-                have = [(a[0], a[1], g) in zf_codes and (first, g) in w_done and (first + 1, g) in w_done for g in range(GROUPS)]
-            else:
-                have = [("z", b, c, 0) in quantized and ("z", b, c, 1) in quantized and ("x", b, a * P // X_PIECE, 0) in quantized for b in range(B)]
-            return (have + [False]).index(False), len(have)
+        def run_tiles(budget, engines):
+            stored = 0
+            for tile in list(tiles_left):
+                ready, total = passes_ready(tile)
+                done = opened[tile][2] if tile in opened else 0
+                if ready == total and budget >= total - done and (tile in opened or free_banks):
+                    matmuls(tile, total, total)
+                    budget = budget - (total - done)
+                    tiles_left.remove(tile)
+                    store(tile, engines[stored % len(engines)])
+                    stored = stored + 1
+            for tile in tiles_left[:OPEN_AHEAD]:
+                ready, total = passes_ready(tile)
+                done = opened[tile][2] if tile in opened else 0
+                if done < ready < total and budget >= ready - done and (tile in opened or len(free_banks) > SPARE_BANKS):
+                    matmuls(tile, ready, total)
+                    budget = budget - (ready - done)
 
-        def run_jobs(budget, fillers, tail, hold=False):
-            n = 0
-            for job in list(jobs):
-                have, need = available(job)
-                done = opened[job][2] if job in opened else 0
-                if have == need and budget >= need - done and (job in opened or free_banks):
-                    matmuls(job)
-                    budget = budget - (need - done)
-                    jobs.remove(job)
-                    if hold and not held:
-                        held.append(job)
-                    else:
-                        store(job, "vector" if tail and n % TAIL_V == 0 else "scalar")
-                    n = n + 1
-                    if fillers and n % FILL_EVERY == 0:
-                        fillers.pop(0)()
-            for job in jobs[:AHEAD]:
-                have, need = available(job)
-                done = opened[job][2] if job in opened else 0
-                if done < have < need and budget >= have - done and (job in opened or len(free_banks) > RESERVE):
-                    matmuls(job, have)
-                    budget = budget - (have - done)
-            while fillers:
-                fillers.pop(0)()
+        x_first = [[("x", b, n) for n in range(BANK // PIECE)] for b in range(B)]
+        x_later = [("x", b, n) for n in range(BANK // PIECE, E // PIECE) for b in range(B)]
+        first_window = w_pieces((0, 1))
+        due = {
+            0: x_first[0],
+            1: x_first[1] + first_window[0:2],
+            2: first_window[2:4],
+            3: first_window[4:6] + dz_halves(0, 0),
+            FIRST_ROW_STEP: x_later[0:3],
+            FIRST_ROW_STEP + 1: x_later[3:6],
+            FIRST_ROW_STEP + 2: w_pieces((2, 3)),
+            FIRST_ROW_STEP + 3: w_pieces((4,)),
+            LAST - 1: dz_halves(0, 2),
+        }
+        long_steps = (FIRST_ROW_STEP + 2, FIRST_ROW_STEP + 3)
+        scalar_pieces = dz_halves(0, 0) + x_first[1] + x_later + dz_halves(0, 2)
+        w_left = w_pieces(range(W_PAIRS))
+        dz_complete = set()
 
-        nc.vector.memset(warm[:], 0.0)
-        nc.scalar.activation(out=warm[:], in_=warm[:], func=ACT.Sin)
-        w_now, z_todo, held, w_held = [], [], [], []
-        group(x_todo[0], "scalar")
+        first_banks = [turn_w(0, 0), turn_w(0, 1)]
+        empty_w(0, 0, first_banks[0])
         build_table()
-        group(x_todo[1], "gpsimd")
-        group(x_todo[2], "scalar")
-        group(x_todo[3], "scalar")
-        s_due, s_next, x_todo = x_todo[0:2], x_todo[2:4], x_todo[4:]
-        last = len(UNITS)
-        for u in range(last):
-            multiply(u, 0)
-            if w_held:
-                item = w_held.pop()
-                w_turned[item] = empty_pair(w_turned[item][0], w_turned[item][1], "vector")
-                w_now.append(item)
-            elif held:
-                store(held.pop(), "vector")
-            hurried = []
-            if u > 0:
-                turn_dz(u - 1)
-                for b, g in reversed(token_done[u - 1]):
-                    (hurried if b == 1 else z_todo).extend(("z", b, g, half) for half in range(2))
-                if hurried:
-                    group(hurried[1], "scalar")
-                    group(hurried[0], "vector")
-                empty_dz(u - 1, "scalar")
-            if u < last - 1:
-                for item in s_due:
-                    quantize_grouped(item)
-            if u > 1:
-                quantize_features(u - 2)
-            for item in hurried:
-                quantize_grouped(item)
-            for n in range(min(QW_STEP[u], len(w_now))):
-                quantize_w(*w_now[0])
-                w_done.add(w_now.pop(0))
-            multiply(u, 1)
-            if u == last - 1:
-                quantize_grouped(s_due.pop())
-            rotate(u, nc.gpsimd if u < G_UNITS else nc.vector)
-            if u < last - 1:
-                s_due, s_next = s_next, []
-            for n in range(S_STEP[u]):
-                if x_todo or z_todo:
-                    s_next.append(z_todo.pop(0) if z_todo else x_todo.pop(0))
-            fillers = [lambda item=item: group(item, "scalar") for item in s_next]
-            for n in range(min(W_STEP[u], len(w_todo))):
-                item = w_todo.pop(0)
-                turn_w(*item)
-                if n == 0:
-                    w_held.append(item)
-                else:
-                    empty_w(*item)
-                    w_now.append(item)
-                if fillers:
-                    fillers.pop(0)()
-            run_jobs(BUDGET[u], fillers, False, not w_held)
-        while held:
-            store(held.pop(), "scalar")
-        urgent = [("z", b, g, half) for b, g in token_done[last - 1] for half in range(2)]
-        turn_dz(last - 1)
-        group(urgent[1], "scalar")
-        quantize_grouped(s_due.pop())
-        group(urgent[0], "vector")
-        empty_dz(last - 1, "scalar")
-        quantize_features(last - 2)
+        empty_w(0, 1, first_banks[1])
+        w_left = w_left[2:]
+        interleave(x_first[0][0], "scalar")
+        interleave(x_first[0][1], "gpsimd")
+
+        for step in range(len(STEPS)):
+            before = step - 1
+            multiply(step, False)
+            if 0 <= step - 2 < FIRST_ROW_STEP:
+                empty_dz(step - 2, "vector")
+            waiting = list(due.get(step, []))
+            if step > 0:
+                upper_half(before, nc.vector, slice(gpsimd_heads(before), None))
+                turn_dz(before)
+                if FIRST_ROW_STEP <= before < LAST - 1:
+                    empty_dz(before, "scalar")
+            if step > 0 and STEPS[before][0] == B - 1 and groups_done[before]:
+                halves = dz_halves(B - 1, groups_done[before][0])
+                interleave(halves[1], "vector")
+                quantize_features(step - 2)
+                interleave(halves[0], "vector")
+                waiting = halves + waiting
+            else:
+                if waiting:
+                    quantize_piece(waiting.pop(0))
+                if step > 1 and before not in long_steps:
+                    quantize_features(step - 2)
+            for piece in waiting:
+                quantize_piece(piece)
+            if step in long_steps:
+                quantize_features(before)
+            multiply(step, True)
+            if step < LAST:
+                lower_half(step, nc.gpsimd)
+                if gpsimd_heads(step):
+                    upper_half(step, nc.gpsimd, slice(0, gpsimd_heads(step)))
+            else:
+                lower_half(step, nc.vector)
+                upper_half(step, nc.vector, slice(0, None))
+
+            copies = [piece for piece in scalar_pieces if piece[0] == "x" or piece[1:3] in dz_complete]
+            copies = copies[:COPIES_PER_STEP]
+            scalar_pieces = [piece for piece in scalar_pieces if piece not in copies]
+            dz_complete.update((STEPS[step][0], g) for g in groups_done[step])
+            if step >= 2:
+                for piece in copies:
+                    interleave(piece, "scalar")
+                copies = []
+            count = W_BANKS_PER_STEP + 2 if step == 0 else W_BANKS_PER_STEP
+            for piece in w_left[:count]:
+                empty_w(piece[1], piece[2], turn_w(piece[1], piece[2]))
+                if copies:
+                    interleave(copies.pop(0), "scalar")
+            w_left = w_left[count:]
+            run_tiles(PASSES_PER_STEP, ["scalar"])
+
+        last_group = groups_done[LAST][0]
+        halves = dz_halves(B - 1, last_group) + dz_halves(0, last_group)
+        empty_dz(LAST - 1, "vector")
+        turn_dz(LAST)
         free_banks.append(0)
-        for item in urgent:
-            quantize_grouped(item)
-        run_jobs(TAIL_A, [], False)
-        quantize_features(last - 1)
-        jobs[:] = sorted(jobs, key=lambda job: job[0] == "dx" and job[1][1] >= 2)
-        run_jobs(999, [], True)
-        assert not jobs and not x_todo and not z_todo
+        run_tiles(PASSES_PER_STEP, ["scalar"])
+        for piece in halves:
+            interleave(piece, "vector")
+        for piece in halves:
+            quantize_piece(piece)
+        empty_dz(LAST, "vector")
+        quantize_features(LAST - 1)
+        quantize_features(LAST)
+        tiles_left[:] = sorted(tiles_left, key=lambda tile: tile[0] == "dx")
+        run_tiles(len(tiles_left) * GROUPS, ["vector", "scalar"])
+        assert not tiles_left and not scalar_pieces and not w_left

@@ -43,12 +43,15 @@ STEPS = (
 FIRST_ROW_STEP = 2 * B
 LAST = len(STEPS) - 1
 
-W_BANKS_PER_STEP = 3
+KEPT_STEP = FIRST_ROW_STEP - 1
+SCALAR_EMPTIES_FROM = FIRST_ROW_STEP + 1
+
+W_BANKS_PER_STEP = 4
 COPIES_PER_STEP = 2
-PASSES_PER_STEP = 12
+PASSES_PER_STEP = 13
 OPEN_AHEAD = 5
 SPARE_BANKS = 2
-VECTOR_HEADS = 2
+PACKED_BUFS = {"w_packed": 6, "tokens_packed": 5, "dz_packed": 3, "dz_kept": 1}
 
 
 def tile_multiqueryattention_pa_v_kernel(tc, x, w_attn, grad_0, grad_1, grad_2, out_0, out_1):
@@ -102,11 +105,11 @@ def tile_multiqueryattention_pa_v_kernel(tc, x, w_attn, grad_0, grad_1, grad_2, 
                 w_rows[r] = keep.tile([P, J], BF16, name="w_rows", tag="w_then_results", bufs=E_TILES)
                 nc.sync.dma_start(out=w_rows[r][:], in_=w_attn[r * P : (r + 1) * P, :])
 
-        load_w(0)
         load_first_group(0)
         load_x(0, 0)
-        load_w(1)
+        load_w(0)
         load_x(1, 0)
+        load_w(1)
         load_w(2)
         load_first_group(1)
         load_x(0, 1)
@@ -119,10 +122,11 @@ def tile_multiqueryattention_pa_v_kernel(tc, x, w_attn, grad_0, grad_1, grad_2, 
         load_later_groups(1)
 
         ident = keep.tile([P, P], F32, name="ident")
-        positions = keep.tile([P, T], F32, name="positions")
+        scratch = ring.tile([P, 4, T], F32, name="scratch", tag="products")
+        positions, turns, minus_rest, waves = [scratch[:, n, :] for n in range(4)]
         make_identity(nc, ident[:])
         nc.gpsimd.iota(
-            positions[:],
+            positions,
             pattern=[[1, SLOTS], [SLOTS, P]],
             base=0,
             channel_multiplier=0,
@@ -136,23 +140,20 @@ def tile_multiqueryattention_pa_v_kernel(tc, x, w_attn, grad_0, grad_1, grad_2, 
         nc.scalar.activation(out=phase[HALF:P, :], in_=phase[HALF:P, :], func=ACT.Sin)
 
         def build_table():
-            split = 8
             one = keep.tile([P, 1], F32, name="one")
-            factors = keep.tile([P, 2 * split], F32, name="factors")
+            ratio = keep.tile([P, 1], F32, name="ratio")
             all_freqs = keep.tile([P, HALF], F32, name="all_freqs")
             masked = keep.tile([P, P], F32, name="masked")
             freq = keep.tile([P, 1], F32, name="freq")
             nc.vector.memset(one[:], 1.0)
-            for a in range(split):
-                coarse = ROPE_BASE ** (-4.0 * split * a / HD)
-                fine = ROPE_BASE ** (-(4.0 * a + 1.0) / HD) / (2.0 * math.pi)
-                nc.vector.tensor_scalar(factors[:, a : a + 1], one[:], coarse, None, ALU.mult)
-                nc.vector.tensor_scalar(factors[:, split + a : split + a + 1], one[:], fine, None, ALU.mult)
-            nc.vector.tensor_tensor(
-                out=all_freqs[:].rearrange("p (a c) -> p a c", a=split),
-                in0=factors[:, 0:split].unsqueeze(2).to_broadcast([P, split, split]),
-                in1=factors[:, split:].unsqueeze(1).to_broadcast([P, split, split]),
-                op=ALU.mult,
+            nc.vector.tensor_scalar(ratio[:], one[:], ROPE_BASE ** (-4.0 / HD), None, ALU.mult)
+            nc.vector.tensor_tensor_scan(
+                out=all_freqs[:],
+                data0=ratio[:].to_broadcast([P, HALF]),
+                data1=one[:].to_broadcast([P, HALF]),
+                initial=ROPE_BASE ** (3.0 / HD) / (2.0 * math.pi),
+                op0=ALU.mult,
+                op1=ALU.mult,
             )
             nc.vector.scalar_tensor_tensor(
                 out=masked[:].rearrange("p (s j) -> p s j", s=2),
@@ -164,9 +165,7 @@ def tile_multiqueryattention_pa_v_kernel(tc, x, w_attn, grad_0, grad_1, grad_2, 
                 accum_out=freq[:],
             )
             halves = (slice(0, T // 2), slice(T // 2, T))
-            turns = keep.tile([P, T], F32, name="turns")
             whole = keep.tile([P, T], I32, name="whole")
-            minus_rest = keep.tile([P, T], F32, name="minus_rest")
             for s in halves:
                 nc.vector.tensor_scalar(turns[:, s], positions[:, s], freq[:], phase[:], ALU.mult, ALU.add)
             for s in halves:
@@ -175,7 +174,6 @@ def tile_multiqueryattention_pa_v_kernel(tc, x, w_attn, grad_0, grad_1, grad_2, 
                 nc.vector.scalar_tensor_tensor(
                     minus_rest[:, s], whole[:, s], ROUNDING, turns[:, s], ALU.subtract, ALU.subtract
                 )
-            waves = keep.tile([P, T], F32, name="waves")
             for s in halves:
                 nc.scalar.activation(out=waves[:, s], in_=minus_rest[:, s], func=ACT.Sin, scale=-2.0 * math.pi)
             for i in range(SLOTS):
@@ -203,16 +201,16 @@ def tile_multiqueryattention_pa_v_kernel(tc, x, w_attn, grad_0, grad_1, grad_2, 
             if last_head:
                 parts = [(len(slots) - 1, count - 1, count)]
             else:
-                products[step] = ring.tile([P, 4 * BANK], F32, name="products")
+                products[step] = ring.tile([P, 4 * BANK], F32, name="products", tag="products")
                 parts = [(n, 0, count) for n in range(len(slots) - 1)] + [(len(slots) - 1, 0, count - 1)]
             for n, lo, hi in parts:
                 i = slots[n]
                 out = products[step][:, n * 2 * BANK : n * 2 * BANK + 2 * count * HD]
-                waves = table[:, i * P : (i + 1) * P].rearrange("p (s j) -> p s j", s=2)
+                cos_sin = table[:, i * P : (i + 1) * P].rearrange("p (s j) -> p s j", s=2)
                 nc.vector.tensor_tensor(
                     out=out.rearrange("p (s h d) -> p s h d", s=2, h=count)[:, :, lo:hi, :],
                     in0=heads[:, lo:hi, i, :].unsqueeze(1).to_broadcast([P, 2, hi - lo, HD]),
-                    in1=waves.unsqueeze(2).to_broadcast([P, 2, 2 * (hi - lo), HALF]),
+                    in1=cos_sin.unsqueeze(2).to_broadcast([P, 2, 2 * (hi - lo), HALF]),
                     op=ALU.mult,
                 )
 
@@ -228,16 +226,14 @@ def tile_multiqueryattention_pa_v_kernel(tc, x, w_attn, grad_0, grad_1, grad_2, 
             by_cos, by_sin, dz = rotation_views(step)
             engine.tensor_tensor(out=dz[:, :, :, 0, :], in0=by_cos[:, :, :, 0, :], in1=by_sin[:, :, :, 1, :], op=ALU.add)
 
-        def upper_half(step, engine, heads):
+        def upper_half(step, engine):
             by_cos, by_sin, dz = rotation_views(step)
             engine.tensor_tensor(
-                out=dz[:, :, heads, 1, :], in0=by_cos[:, :, heads, 1, :], in1=by_sin[:, :, heads, 0, :], op=ALU.subtract
+                out=dz[:, :, :, 1, :], in0=by_cos[:, :, :, 1, :], in1=by_sin[:, :, :, 0, :], op=ALU.subtract
             )
 
-        def gpsimd_heads(step):
-            if 0 < step <= FIRST_ROW_STEP:
-                return rotated_heads(STEPS[step][2]) - VECTOR_HEADS // len(STEPS[step][1])
-            return 0
+        def gpsimd_takes_both(step):
+            return 0 <= step - 1 < SCALAR_EMPTIES_FROM
 
         def copy_on(engine, out, in_):
             if engine == "vector":
@@ -255,16 +251,14 @@ def tile_multiqueryattention_pa_v_kernel(tc, x, w_attn, grad_0, grad_1, grad_2, 
                     nc.tensor.transpose(bank[:, (2 * n + u) * P : (2 * n + u + 1) * P], words[:, u::2], ident[:])
             return number, bank
 
-        def empty_words(filled, engine, name, bufs):
+        def empty_words(filled, engine, packed):
             number, bank = filled
-            packed = ring.tile([P, 2 * BANK], BF16, name=name, align_bytes=64, bufs=bufs)
             copy_on(
                 engine,
-                packed[:].bitcast(F32).rearrange("p (n r u) -> p n r u", n=2, u=2),
+                packed.bitcast(F32).rearrange("p (n r u) -> p n r u", n=2, u=2),
                 bank[:].rearrange("p (n u r) -> p n r u", n=2, u=2),
             )
             free_banks.append(number)
-            return packed
 
         def mx_tiles(name, width):
             codes = keep.tile([P, width], U32, name=name + "_codes", align_bytes=64)
@@ -273,14 +267,14 @@ def tile_multiqueryattention_pa_v_kernel(tc, x, w_attn, grad_0, grad_1, grad_2, 
 
         def quantize(target, columns, dtype, packed):
             codes, scales = target
-            nc.vector.quantize_mx(out=codes[:, columns].bitcast(dtype), scales=scales[:, columns], in_=packed[:])
+            nc.vector.quantize_mx(out=codes[:, columns].bitcast(dtype), scales=scales[:, columns], in_=packed)
 
         x_mx = [mx_tiles("x%d" % b, E) for b in range(B)]
         w_mx = [mx_tiles("w%d" % g, E) for g in range(GROUPS)]
         dz_token_mx = {(b, g): mx_tiles("dz_token%d_%d" % (b, g), BANK) for b in range(B) for g in range(GROUPS)}
         dz_feature_mx = {}
         quantized = set()
-        dz_banks, dz_packed, w_packed, piece_packed = {}, {}, {}, {}
+        dz_banks, dz_packed, packed = {}, {}, {}
 
         def blocks(step):
             b, slots, groups = STEPS[step]
@@ -291,11 +285,13 @@ def tile_multiqueryattention_pa_v_kernel(tc, x, w_attn, grad_0, grad_1, grad_2, 
             dz_banks[step] = transpose_words(first, second)
 
         def empty_dz(step, engine):
-            dz_packed[step] = empty_words(dz_banks[step], engine, "dz_packed", 3)
+            name = "dz_kept" if step == KEPT_STEP else "dz_packed"
+            dz_packed[step] = ring.tile([P, 2 * BANK], BF16, name=name, align_bytes=64, bufs=PACKED_BUFS[name])
+            empty_words(dz_banks[step], engine, dz_packed[step][:])
 
         def quantize_features(step):
             codes, scales = mx_tiles("dz_feature%d" % step, 2 * P)
-            quantize((codes, scales), slice(0, 2 * P), E5M2, dz_packed[step])
+            quantize((codes, scales), slice(0, 2 * P), E5M2, dz_packed[step][:])
             for n, block in enumerate(blocks(step)):
                 dz_feature_mx[block] = (codes[:, n * P : (n + 1) * P], scales[:, n * P : (n + 1) * P])
 
@@ -303,50 +299,53 @@ def tile_multiqueryattention_pa_v_kernel(tc, x, w_attn, grad_0, grad_1, grad_2, 
             columns = slice(g * BANK, (g + 1) * BANK)
             return transpose_words(w_rows[2 * pair][:, columns], w_rows[2 * pair + 1][:, columns])
 
-        def empty_w(pair, g, filled):
-            w_packed[pair, g] = empty_words(filled, "scalar", "w_packed", 11)
+        def operand_columns(operand):
+            if operand[0] == "dz":
+                return slice(0, BANK)
+            part = operand[1] if operand[0] == "w" else operand[2]
+            return slice(part * BANK, min((part + 1) * BANK, E))
 
-        def interleave(piece, engine):
-            if piece[0] == "x":
-                part, lo = divmod(piece[2] * PIECE, BANK)
-                rows = x_rows[piece[1], part][:, :, lo : lo + PIECE]
-            else:
-                rows = dz_slots(piece[1], (piece[2],))[:, :, piece[3] * PIECE : (piece[3] + 1) * PIECE]
-            piece_packed[piece] = ring.tile([P, SLOTS * PIECE], BF16, name="piece_packed", align_bytes=64, bufs=9)
+        def packed_tile(operand):
+            if operand not in packed:
+                name = "w_packed" if operand[0] == "w" else "tokens_packed"
+                packed[operand] = ring.tile([P, SLOTS * BANK], BF16, name=name, align_bytes=64, bufs=PACKED_BUFS[name])
+            return packed[operand]
+
+        def empty_w(pair, g, filled):
+            part, half = divmod(pair, 2)
+            empty_words(filled, "scalar", packed_tile(("w", part, g))[:, half * 2 * BANK : (half + 1) * 2 * BANK])
+
+        def interleave(operand, lo, hi, engine):
+            rows = x_rows[operand[1:]] if operand[0] == "x" else dz_slots(operand[1], operand[2:])
             copy_on(
                 engine,
-                piece_packed[piece][:].rearrange("p (c n i) -> p c i n", n=4, i=SLOTS),
-                rows.rearrange("p i (c n) -> p c i n", n=4),
+                packed_tile(operand)[:, SLOTS * lo : SLOTS * hi].rearrange("p (c n i) -> p c i n", n=4, i=SLOTS),
+                rows[:, :, lo:hi].rearrange("p i (c n) -> p c i n", n=4),
             )
 
-        def quantize_piece(piece):
-            if piece[0] == "w":
-                pair, g = piece[1:]
-                quantize(w_mx[g], slice(pair * 2 * P, (pair + 1) * 2 * P), E4M3, w_packed[pair, g])
-            elif piece[0] == "x":
-                quantize(x_mx[piece[1]], slice(piece[2] * PIECE, (piece[2] + 1) * PIECE), E4M3, piece_packed[piece])
+        def quantize_operand(operand):
+            columns = operand_columns(operand)
+            source = packed[operand][:, 0 : SLOTS * (columns.stop - columns.start)]
+            if operand[0] == "w":
+                quantize(w_mx[operand[2]], columns, E4M3, source)
+            elif operand[0] == "x":
+                quantize(x_mx[operand[1]], columns, E4M3, source)
             else:
-                target = dz_token_mx[piece[1], piece[2]]
-                quantize(target, slice(piece[3] * PIECE, (piece[3] + 1) * PIECE), E5M2, piece_packed[piece])
-            quantized.add(piece)
-
-        def dz_halves(b, g):
-            return [("dz", b, g, half) for half in range(BANK // PIECE)]
-
-        def w_pieces(pairs):
-            return [("w", pair, g) for pair in pairs for g in range(GROUPS)]
+                quantize(dz_token_mx[operand[1:]], columns, E5M2, source)
+            quantized.add(operand)
 
         opened = {}
 
         def passes_ready(tile):
             if tile[0] == "dx":
-                pair = WINDOWS[tile[3]][0] // (2 * P)
+                first = WINDOWS[tile[3]][0]
+                parts = range(first // BANK, (first + BANK - 1) // BANK + 1)
                 ready = [
-                    (tile[1], tile[2], g) in dz_feature_mx and {("w", pair, g), ("w", pair + 1, g)} <= quantized
+                    (tile[1], tile[2], g) in dz_feature_mx and {("w", part, g) for part in parts} <= quantized
                     for g in range(GROUPS)
                 ]
             else:
-                ready = [set(dz_halves(b, tile[2]) + [("x", b, tile[1] * P // PIECE)]) <= quantized for b in range(B)]
+                ready = [{("dz", b, tile[2]), ("x", b, tile[1] * P // BANK)} <= quantized for b in range(B)]
             return (ready + [False]).index(False), len(ready)
 
         def matmuls(tile, end, total):
@@ -418,97 +417,97 @@ def tile_multiqueryattention_pa_v_kernel(tc, x, w_attn, grad_0, grad_1, grad_2, 
                     matmuls(tile, ready, total)
                     budget = budget - (ready - done)
 
-        x_first = [[("x", b, n) for n in range(BANK // PIECE)] for b in range(B)]
-        x_later = [("x", b, n) for n in range(BANK // PIECE, E // PIECE) for b in range(B)]
-        first_window = w_pieces((0, 1))
         due = {
-            0: x_first[0],
-            1: x_first[1] + first_window[0:2],
-            2: first_window[2:4],
-            3: first_window[4:6] + dz_halves(0, 0),
-            FIRST_ROW_STEP: x_later[0:3],
-            FIRST_ROW_STEP + 1: x_later[3:6],
-            FIRST_ROW_STEP + 2: w_pieces((2, 3)),
-            FIRST_ROW_STEP + 3: w_pieces((4,)),
-            LAST - 1: dz_halves(0, 2),
+            0: [("x", 0, 0)],
+            1: [("x", 1, 0)],
+            2: [("w", 0, 0), ("w", 0, 1)],
+            3: [("w", 0, 2), ("dz", 0, 0)],
+            FIRST_ROW_STEP: [("x", b, 1) for b in range(B)],
+            FIRST_ROW_STEP + 1: [("x", b, 2) for b in range(B)],
+            FIRST_ROW_STEP + 2: [("w", 1, g) for g in range(GROUPS)],
+            FIRST_ROW_STEP + 3: [("w", 2, g) for g in range(GROUPS)],
+            LAST - 1: [("dz", 0, 2)],
         }
         long_steps = (FIRST_ROW_STEP + 2, FIRST_ROW_STEP + 3)
-        scalar_pieces = dz_halves(0, 0) + x_first[1] + x_later + dz_halves(0, 2)
-        w_left = w_pieces(range(W_PAIRS))
+        scalar_operands = [("dz", 0, 0), ("x", 1, 0), ("x", 0, 1), ("x", 1, 1), ("x", 0, 2), ("x", 1, 2), ("dz", 0, 2)]
+        scalar_copies = []
+        for operand in scalar_operands:
+            columns = operand_columns(operand)
+            scalar_copies.extend((operand, lo, lo + PIECE) for lo in range(0, columns.stop - columns.start, PIECE))
+        w_left = [(pair, g) for pair in range(W_PAIRS) for g in range(GROUPS)]
         dz_complete = set()
 
-        first_banks = [turn_w(0, 0), turn_w(0, 1)]
-        empty_w(0, 0, first_banks[0])
         build_table()
-        empty_w(0, 1, first_banks[1])
-        w_left = w_left[2:]
-        interleave(x_first[0][0], "scalar")
-        interleave(x_first[0][1], "gpsimd")
+        interleave(("x", 0, 0), 0, PIECE, "scalar")
+        interleave(("x", 0, 0), PIECE, BANK, "gpsimd")
 
         for step in range(len(STEPS)):
             before = step - 1
             multiply(step, False)
-            if 0 <= step - 2 < FIRST_ROW_STEP:
+            if 0 <= step - 2 < SCALAR_EMPTIES_FROM:
                 empty_dz(step - 2, "vector")
             waiting = list(due.get(step, []))
             if step > 0:
-                upper_half(before, nc.vector, slice(gpsimd_heads(before), None))
+                if not gpsimd_takes_both(before):
+                    upper_half(before, nc.vector)
                 turn_dz(before)
-                if FIRST_ROW_STEP <= before < LAST - 1:
-                    empty_dz(before, "scalar")
             if step > 0 and STEPS[before][0] == B - 1 and groups_done[before]:
-                halves = dz_halves(B - 1, groups_done[before][0])
-                interleave(halves[1], "vector")
-                quantize_features(step - 2)
-                interleave(halves[0], "vector")
-                waiting = halves + waiting
-            else:
-                if waiting:
-                    quantize_piece(waiting.pop(0))
-                if step > 1 and before not in long_steps:
+                operand = ("dz", B - 1, groups_done[before][0])
+                if step == LAST:
+                    interleave(operand, PIECE, BANK, "scalar")
                     quantize_features(step - 2)
-            for piece in waiting:
-                quantize_piece(piece)
+                    interleave(operand, 0, PIECE, "vector")
+                else:
+                    interleave(operand, 0, BANK, "vector")
+                    quantize_features(step - 2)
+                waiting = [operand] + waiting
+            else:
+                if before >= SCALAR_EMPTIES_FROM:
+                    empty_dz(before, "scalar")
+                if waiting:
+                    quantize_operand(waiting.pop(0))
+                if step > 1 and before not in long_steps and step - 2 != KEPT_STEP:
+                    quantize_features(step - 2)
+            for operand in waiting:
+                quantize_operand(operand)
             if step in long_steps:
                 quantize_features(before)
             multiply(step, True)
             if step < LAST:
                 lower_half(step, nc.gpsimd)
-                if gpsimd_heads(step):
-                    upper_half(step, nc.gpsimd, slice(0, gpsimd_heads(step)))
+                if gpsimd_takes_both(step):
+                    upper_half(step, nc.gpsimd)
             else:
                 lower_half(step, nc.vector)
-                upper_half(step, nc.vector, slice(0, None))
+                upper_half(step, nc.vector)
 
-            copies = [piece for piece in scalar_pieces if piece[0] == "x" or piece[1:3] in dz_complete]
+            copies = [copy for copy in scalar_copies if copy[0][0] == "x" or copy[0][1:] in dz_complete]
             copies = copies[:COPIES_PER_STEP]
-            scalar_pieces = [piece for piece in scalar_pieces if piece not in copies]
+            scalar_copies = [copy for copy in scalar_copies if copy not in copies]
             dz_complete.update((STEPS[step][0], g) for g in groups_done[step])
             if step >= 2:
-                for piece in copies:
-                    interleave(piece, "scalar")
+                for copy in copies:
+                    interleave(*copy, "scalar")
                 copies = []
-            count = W_BANKS_PER_STEP + 2 if step == 0 else W_BANKS_PER_STEP
-            for piece in w_left[:count]:
-                empty_w(piece[1], piece[2], turn_w(piece[1], piece[2]))
+            for pair, g in w_left[:W_BANKS_PER_STEP]:
+                empty_w(pair, g, turn_w(pair, g))
                 if copies:
-                    interleave(copies.pop(0), "scalar")
-            w_left = w_left[count:]
+                    interleave(*copies.pop(0), "scalar")
+            w_left = w_left[W_BANKS_PER_STEP:]
             run_tiles(PASSES_PER_STEP, ["scalar"])
 
-        last_group = groups_done[LAST][0]
-        halves = dz_halves(B - 1, last_group) + dz_halves(0, last_group)
-        empty_dz(LAST - 1, "vector")
+        last_operands = [("dz", b, groups_done[LAST][0]) for b in range(B)]
         turn_dz(LAST)
         free_banks.append(0)
         run_tiles(PASSES_PER_STEP, ["scalar"])
-        for piece in halves:
-            interleave(piece, "vector")
-        for piece in halves:
-            quantize_piece(piece)
+        for operand in last_operands:
+            interleave(operand, 0, BANK, "vector")
+        for operand in last_operands:
+            quantize_operand(operand)
+        empty_dz(LAST - 1, "vector")
         empty_dz(LAST, "vector")
-        quantize_features(LAST - 1)
-        quantize_features(LAST)
+        for step in (KEPT_STEP, LAST - 1, LAST):
+            quantize_features(step)
         tiles_left[:] = sorted(tiles_left, key=lambda tile: tile[0] == "dx")
         run_tiles(len(tiles_left) * GROUPS, ["vector", "scalar"])
-        assert not tiles_left and not scalar_pieces and not w_left
+        assert not tiles_left and not scalar_copies and not w_left

import math
from contextlib import ExitStack

import concourse.mybir as mybir
from concourse.masks import make_identity

B, T, E, H, HD = 2, 512, 1280, 10, 128
J = (H + 2) * HD
ROPE_BASE = 10000.0
FLOPS = 2 * 2 * B * T * E * J

F32 = mybir.dt.float32
BF16 = mybir.dt.bfloat16
I32 = mybir.dt.int32
U32 = mybir.dt.uint32
U8 = mybir.dt.uint8
E4M3 = mybir.dt.float8_e4m3fn_x4
E5M2 = mybir.dt.float8_e5m2_x4
ALU = mybir.AluOpType
ACT = mybir.ActivationFunctionType

P = 128
SLOTS = 4
HALF = HD // 2
BANK = 512
BANKS = 8
GROUPS = J // BANK
GROUP_HEADS = BANK // HD
LATER_HEADS = H + 1 - GROUP_HEADS
E_TILES = E // P
W_PAIRS = E_TILES // 2
PIECE = 256
X_LOADS = ((0, 512), (512, 1024), (1024, E))
WINDOWS = ((0, 0), (512, 512), (E - BANK, 1024))
ROUNDING = 1.5 * 2.0**23

STEPS = (
    [(b, (i, i + 1), (0,)) for b in range(B) for i in (0, 2)]
    + [(0, (i,), (1, 2)) for i in range(SLOTS)]
    + [(1, (i,), (1, 2)) for i in (0, 1)]
    + [(1, (2, 3), (g,)) for g in (2, 1)]
)
FIRST_ROW_STEP = 2 * B
LAST = len(STEPS) - 1

KEPT_STEP = FIRST_ROW_STEP - 1
SCALAR_EMPTIES_FROM = FIRST_ROW_STEP + 1

W_BANKS_PER_STEP = 4
COPIES_PER_STEP = 2
PASSES_PER_STEP = 13
OPEN_AHEAD = 5
SPARE_BANKS = 2
PACKED_BUFS = {"w_packed": 6, "tokens_packed": 5, "dz_packed": 3, "dz_kept": 1}


def tile_multiqueryattention_pa_v_kernel(tc, x, w_attn, grad_0, grad_1, grad_2, out_0, out_1):
    nc = tc.nc

    with ExitStack() as ctx:
        keep = ctx.enter_context(tc.tile_pool(name="keep", bufs=1))
        ring = ctx.enter_context(tc.tile_pool(name="ring", bufs=2))
        psum = ctx.enter_context(tc.psum_pool(name="psum", bufs=1))
        ctx.enter_context(tc.manual_schedule())

        free_banks = list(range(1, BANKS))

        def take_bank():
            number = free_banks.pop(0)
            return number, psum.tile([P, BANK], F32, name="bank", tag="bank%d" % number)

        grad_first, grad_later, x_rows, w_rows = {}, {}, {}, {}
        dz_first = [keep.tile([P, SLOTS * BANK], BF16, name="dz_first%d" % b, align_bytes=64) for b in range(B)]
        dz_later = [keep.tile([P, SLOTS * 2 * BANK], BF16, name="dz_later%d" % b, align_bytes=64) for b in range(B)]

        def load_first_group(b):
            grad_first[b] = keep.tile([P, GROUP_HEADS * T], BF16, name="grad_first%d" % b)
            nc.sync.dma_start(
                out=grad_first[b][:].rearrange("p (h c) -> p h c", h=GROUP_HEADS),
                in_=grad_0[b, 0:GROUP_HEADS].rearrange("h (p i) d -> p h (i d)", i=SLOTS),
            )

        def load_later_groups(b):
            query_heads = H - GROUP_HEADS
            grad_later[b] = keep.tile([P, LATER_HEADS * T], BF16, name="grad_later%d" % b)
            nc.sync.dma_start(
                out=grad_later[b][:, 0 : query_heads * T].rearrange("p (h c) -> p h c", h=query_heads),
                in_=grad_0[b, GROUP_HEADS:H].rearrange("h (p i) d -> p h (i d)", i=SLOTS),
            )
            nc.sync.dma_start(
                out=grad_later[b][:, query_heads * T :], in_=grad_1[b, 0].rearrange("(p i) d -> p (i d)", i=SLOTS)
            )
            nc.sync.dma_start(
                out=dz_later[b][:].rearrange("p (i c) -> p i c", i=SLOTS)[:, :, LATER_HEADS * HD :],
                in_=grad_2[b, 0].rearrange("(p i) d -> p i d", i=SLOTS),
            )

        def load_x(b, part):
            lo, hi = X_LOADS[part]
            x_rows[b, part] = keep.tile([P, SLOTS, hi - lo], BF16, name="x_rows%d_%d" % (b, part))
            nc.sync.dma_start(out=x_rows[b, part][:], in_=x[b].rearrange("(p i) e -> p i e", i=SLOTS)[:, :, lo:hi])

        def load_w(pair):
            for r in (2 * pair, 2 * pair + 1):
                w_rows[r] = keep.tile([P, J], BF16, name="w_rows", tag="w_then_results", bufs=E_TILES)
                nc.sync.dma_start(out=w_rows[r][:], in_=w_attn[r * P : (r + 1) * P, :])

        load_first_group(0)
        load_x(0, 0)
        load_w(0)
        load_x(1, 0)
        load_w(1)
        load_w(2)
        load_first_group(1)
        load_x(0, 1)
        load_x(1, 1)
        load_w(3)
        load_w(4)
        load_later_groups(0)
        load_x(0, 2)
        load_x(1, 2)
        load_later_groups(1)

        ident = keep.tile([P, P], F32, name="ident")
        scratch = ring.tile([P, 4, T], F32, name="scratch", tag="products")
        positions, turns, minus_rest, waves = [scratch[:, n, :] for n in range(4)]
        make_identity(nc, ident[:])
        nc.gpsimd.iota(
            positions,
            pattern=[[1, SLOTS], [SLOTS, P]],
            base=0,
            channel_multiplier=0,
            allow_small_or_imprecise_dtypes=True,
        )
        table = psum.tile([P, BANK], F32, name="table", tag="bank0")

        phase = keep.tile([P, 1], F32, name="phase")
        nc.vector.memset(phase[0:HALF, :], 0.25)
        nc.vector.memset(phase[HALF:P, :], 0.0)
        nc.scalar.activation(out=phase[HALF:P, :], in_=phase[HALF:P, :], func=ACT.Sin)

        def build_table():
            one = keep.tile([P, 1], F32, name="one")
            ratio = keep.tile([P, 1], F32, name="ratio")
            all_freqs = keep.tile([P, HALF], F32, name="all_freqs")
            masked = keep.tile([P, P], F32, name="masked")
            freq = keep.tile([P, 1], F32, name="freq")
            nc.vector.memset(one[:], 1.0)
            nc.vector.tensor_scalar(ratio[:], one[:], ROPE_BASE ** (-4.0 / HD), None, ALU.mult)
            nc.vector.tensor_tensor_scan(
                out=all_freqs[:],
                data0=ratio[:].to_broadcast([P, HALF]),
                data1=one[:].to_broadcast([P, HALF]),
                initial=ROPE_BASE ** (3.0 / HD) / (2.0 * math.pi),
                op0=ALU.mult,
                op1=ALU.mult,
            )
            nc.vector.scalar_tensor_tensor(
                out=masked[:].rearrange("p (s j) -> p s j", s=2),
                in0=ident[:].rearrange("p (s j) -> p s j", s=2),
                scalar=1.0,
                in1=all_freqs[:].unsqueeze(1).to_broadcast([P, 2, HALF]),
                op0=ALU.mult,
                op1=ALU.mult,
                accum_out=freq[:],
            )
            halves = (slice(0, T // 2), slice(T // 2, T))
            whole = keep.tile([P, T], I32, name="whole")
            for s in halves:
                nc.vector.tensor_scalar(turns[:, s], positions[:, s], freq[:], phase[:], ALU.mult, ALU.add)
            for s in halves:
                nc.vector.tensor_scalar(whole[:, s], turns[:, s], ROUNDING, None, ALU.add)
            for s in halves:
                nc.vector.scalar_tensor_tensor(
                    minus_rest[:, s], whole[:, s], ROUNDING, turns[:, s], ALU.subtract, ALU.subtract
                )
            for s in halves:
                nc.scalar.activation(out=waves[:, s], in_=minus_rest[:, s], func=ACT.Sin, scale=-2.0 * math.pi)
            for i in range(SLOTS):
                nc.tensor.transpose(table[:, i * P : (i + 1) * P], waves[:, i * P : (i + 1) * P], ident[:])

        products = {}

        def dz_slots(b, groups):
            if groups[0] == 0:
                return dz_first[b][:].rearrange("p (i c) -> p i c", i=SLOTS)
            lo = (groups[0] - 1) * BANK
            return dz_later[b][:].rearrange("p (i c) -> p i c", i=SLOTS)[:, :, lo : lo + BANK * len(groups)]

        def rotated_heads(groups):
            return sum(GROUP_HEADS - 1 if g == GROUPS - 1 else GROUP_HEADS for g in groups)

        def multiply(step, last_head):
            b, slots, groups = STEPS[step]
            count = rotated_heads(groups)
            if groups[0] == 0:
                heads = grad_first[b][:].rearrange("p (h i d) -> p h i d", h=GROUP_HEADS, i=SLOTS)
            else:
                first = GROUP_HEADS * (groups[0] - 1)
                heads = grad_later[b][:].rearrange("p (h i d) -> p h i d", h=LATER_HEADS, i=SLOTS)[:, first : first + count]
            if last_head:
                parts = [(len(slots) - 1, count - 1, count)]
            else:
                products[step] = ring.tile([P, 4 * BANK], F32, name="products", tag="products")
                parts = [(n, 0, count) for n in range(len(slots) - 1)] + [(len(slots) - 1, 0, count - 1)]
            for n, lo, hi in parts:
                i = slots[n]
                out = products[step][:, n * 2 * BANK : n * 2 * BANK + 2 * count * HD]
                cos_sin = table[:, i * P : (i + 1) * P].rearrange("p (s j) -> p s j", s=2)
                nc.vector.tensor_tensor(
                    out=out.rearrange("p (s h d) -> p s h d", s=2, h=count)[:, :, lo:hi, :],
                    in0=heads[:, lo:hi, i, :].unsqueeze(1).to_broadcast([P, 2, hi - lo, HD]),
                    in1=cos_sin.unsqueeze(2).to_broadcast([P, 2, 2 * (hi - lo), HALF]),
                    op=ALU.mult,
                )

        def rotation_views(step):
            b, slots, groups = STEPS[step]
            count = rotated_heads(groups)
            both = products[step][:].rearrange("p (n c) -> p n c", n=len(slots))[:, :, 0 : 2 * count * HD]
            both = both.rearrange("p n (s h f j) -> p n s h f j", s=2, h=count, f=2)
            dz = dz_slots(b, groups)[:, slots[0] : slots[0] + len(slots), 0 : count * HD]
            return both[:, :, 0], both[:, :, 1], dz.rearrange("p n (h f j) -> p n h f j", h=count, f=2)

        def lower_half(step, engine):
            by_cos, by_sin, dz = rotation_views(step)
            engine.tensor_tensor(out=dz[:, :, :, 0, :], in0=by_cos[:, :, :, 0, :], in1=by_sin[:, :, :, 1, :], op=ALU.add)

        def upper_half(step, engine):
            by_cos, by_sin, dz = rotation_views(step)
            engine.tensor_tensor(
                out=dz[:, :, :, 1, :], in0=by_cos[:, :, :, 1, :], in1=by_sin[:, :, :, 0, :], op=ALU.subtract
            )

        def gpsimd_takes_both(step):
            return 0 <= step - 1 < SCALAR_EMPTIES_FROM

        def copy_on(engine, out, in_):
            if engine == "vector":
                nc.vector.tensor_copy(out=out, in_=in_)
            elif engine == "scalar":
                nc.scalar.copy(out=out, in_=in_)
            else:
                nc.gpsimd.tensor_scalar(out, in_, 1.0, 0.0, ALU.mult, ALU.add)

        def transpose_words(first, second):
            number, bank = take_bank()
            for n, rows in enumerate((first, second)):
                words = rows.bitcast(F32)
                for u in range(2):
                    nc.tensor.transpose(bank[:, (2 * n + u) * P : (2 * n + u + 1) * P], words[:, u::2], ident[:])
            return number, bank

        def empty_words(filled, engine, packed):
            number, bank = filled
            copy_on(
                engine,
                packed.bitcast(F32).rearrange("p (n r u) -> p n r u", n=2, u=2),
                bank[:].rearrange("p (n u r) -> p n r u", n=2, u=2),
            )
            free_banks.append(number)

        def mx_tiles(name, width):
            codes = keep.tile([P, width], U32, name=name + "_codes", align_bytes=64)
            scales = keep.tile([P, width], U8, name=name + "_scales", align_bytes=64)
            return codes, scales

        def quantize(target, columns, dtype, packed):
            codes, scales = target
            nc.vector.quantize_mx(out=codes[:, columns].bitcast(dtype), scales=scales[:, columns], in_=packed)

        x_mx = [mx_tiles("x%d" % b, E) for b in range(B)]
        w_mx = [mx_tiles("w%d" % g, E) for g in range(GROUPS)]
        dz_token_mx = {(b, g): mx_tiles("dz_token%d_%d" % (b, g), BANK) for b in range(B) for g in range(GROUPS)}
        dz_feature_mx = {}
        quantized = set()
        dz_banks, dz_packed, packed = {}, {}, {}

        def blocks(step):
            b, slots, groups = STEPS[step]
            return [(b, i, g) for i in slots for g in groups]

        def turn_dz(step):
            first, second = [dz_slots(b, (g,))[:, i, :] for b, i, g in blocks(step)]
            dz_banks[step] = transpose_words(first, second)

        def empty_dz(step, engine):
            name = "dz_kept" if step == KEPT_STEP else "dz_packed"
            dz_packed[step] = ring.tile([P, 2 * BANK], BF16, name=name, align_bytes=64, bufs=PACKED_BUFS[name])
            empty_words(dz_banks[step], engine, dz_packed[step][:])

        def quantize_features(step):
            codes, scales = mx_tiles("dz_feature%d" % step, 2 * P)
            quantize((codes, scales), slice(0, 2 * P), E5M2, dz_packed[step][:])
            for n, block in enumerate(blocks(step)):
                dz_feature_mx[block] = (codes[:, n * P : (n + 1) * P], scales[:, n * P : (n + 1) * P])

        def turn_w(pair, g):
            columns = slice(g * BANK, (g + 1) * BANK)
            return transpose_words(w_rows[2 * pair][:, columns], w_rows[2 * pair + 1][:, columns])

        def operand_columns(operand):
            if operand[0] == "dz":
                return slice(0, BANK)
            part = operand[1] if operand[0] == "w" else operand[2]
            return slice(part * BANK, min((part + 1) * BANK, E))

        def packed_tile(operand):
            if operand not in packed:
                name = "w_packed" if operand[0] == "w" else "tokens_packed"
                packed[operand] = ring.tile([P, SLOTS * BANK], BF16, name=name, align_bytes=64, bufs=PACKED_BUFS[name])
            return packed[operand]

        def empty_w(pair, g, filled):
            part, half = divmod(pair, 2)
            empty_words(filled, "scalar", packed_tile(("w", part, g))[:, half * 2 * BANK : (half + 1) * 2 * BANK])

        def interleave(operand, lo, hi, engine):
            rows = x_rows[operand[1:]] if operand[0] == "x" else dz_slots(operand[1], operand[2:])
            copy_on(
                engine,
                packed_tile(operand)[:, SLOTS * lo : SLOTS * hi].rearrange("p (c n i) -> p c i n", n=4, i=SLOTS),
                rows[:, :, lo:hi].rearrange("p i (c n) -> p c i n", n=4),
            )

        def quantize_operand(operand):
            columns = operand_columns(operand)
            source = packed[operand][:, 0 : SLOTS * (columns.stop - columns.start)]
            if operand[0] == "w":
                quantize(w_mx[operand[2]], columns, E4M3, source)
            elif operand[0] == "x":
                quantize(x_mx[operand[1]], columns, E4M3, source)
            else:
                quantize(dz_token_mx[operand[1:]], columns, E5M2, source)
            quantized.add(operand)

        opened = {}

        def passes_ready(tile):
            if tile[0] == "dx":
                first = WINDOWS[tile[3]][0]
                parts = range(first // BANK, (first + BANK - 1) // BANK + 1)
                ready = [
                    (tile[1], tile[2], g) in dz_feature_mx and {("w", part, g) for part in parts} <= quantized
                    for g in range(GROUPS)
                ]
            else:
                ready = [{("dz", b, tile[2]), ("x", b, tile[1] * P // BANK)} <= quantized for b in range(B)]
            return (ready + [False]).index(False), len(ready)

        def matmuls(tile, end, total):
            if tile not in opened:
                opened[tile] = take_bank() + (0,)
            number, bank, done = opened[tile]
            for n in range(done, end):
                if tile[0] == "dx":
                    columns = slice(WINDOWS[tile[3]][0], WINDOWS[tile[3]][0] + BANK)
                    codes, scales = dz_feature_mx[tile[1], tile[2], n]
                    lhs, lhs_scale = codes.bitcast(E5M2), scales
                    rhs, rhs_scale = w_mx[n][0][:, columns].bitcast(E4M3), w_mx[n][1][:, columns]
                else:
                    columns = slice(tile[1] * P, (tile[1] + 1) * P)
                    codes, scales = dz_token_mx[n, tile[2]]
                    lhs, lhs_scale = x_mx[n][0][:, columns].bitcast(E4M3), x_mx[n][1][:, columns]
                    rhs, rhs_scale = codes[:].bitcast(E5M2), scales[:]
                nc.tensor.matmul_mx(
                    out=bank[:],
                    lhsT=lhs,
                    lhsT_scale=lhs_scale,
                    rhs=rhs,
                    rhs_scale=rhs_scale,
                    start=(n == 0),
                    stop=(n == total - 1),
                )
            opened[tile] = (number, bank, end)

        def store(tile, engine):
            number, bank = opened[tile][0:2]
            if tile[0] == "dx":
                first, kept = WINDOWS[tile[3]]
                width = first + BANK - kept
                dest = out_0[tile[1]].rearrange("(p i) e -> p i e", i=SLOTS)[:, tile[2], kept : kept + width]
            else:
                width = BANK
                dest = out_1[tile[1] * P : (tile[1] + 1) * P, tile[2] * BANK : (tile[2] + 1) * BANK]
            result = keep.tile([P, width], F32, name="result", tag="w_then_results", bufs=E_TILES)
            copy_on(engine, result[:], bank[:, BANK - width :])
            free_banks.append(number)
            nc.sync.dma_start(out=dest, in_=result[:])

        tiles_left, groups_done, seen = [], {}, set()
        for step in range(len(STEPS)):
            seen.update(blocks(step))
            b, slots, groups = STEPS[step]
            groups_done[step] = [g for g in groups if {(b, i, g) for i in range(SLOTS)} <= seen]
            for i in slots:
                if {(b, i, g) for g in range(GROUPS)} <= seen:
                    tiles_left.extend(("dx", b, i, window) for window in range(len(WINDOWS)))
            if b == B - 1:
                tiles_left.extend(("dw", r, g) for g in groups_done[step] for r in range(E_TILES))

        def run_tiles(budget, engines):
            stored = 0
            for tile in list(tiles_left):
                ready, total = passes_ready(tile)
                done = opened[tile][2] if tile in opened else 0
                if ready == total and budget >= total - done and (tile in opened or free_banks):
                    matmuls(tile, total, total)
                    budget = budget - (total - done)
                    tiles_left.remove(tile)
                    store(tile, engines[stored % len(engines)])
                    stored = stored + 1
            for tile in tiles_left[:OPEN_AHEAD]:
                ready, total = passes_ready(tile)
                done = opened[tile][2] if tile in opened else 0
                if done < ready < total and budget >= ready - done and (tile in opened or len(free_banks) > SPARE_BANKS):
                    matmuls(tile, ready, total)
                    budget = budget - (ready - done)

        due = {
            0: [("x", 0, 0)],
            1: [("x", 1, 0)],
            2: [("w", 0, 0), ("w", 0, 1)],
            3: [("w", 0, 2), ("dz", 0, 0)],
            FIRST_ROW_STEP: [("x", b, 1) for b in range(B)],
            FIRST_ROW_STEP + 1: [("x", b, 2) for b in range(B)],
            FIRST_ROW_STEP + 2: [("w", 1, g) for g in range(GROUPS)],
            FIRST_ROW_STEP + 3: [("w", 2, g) for g in range(GROUPS)],
            LAST - 1: [("dz", 0, 2)],
        }
        long_steps = (FIRST_ROW_STEP + 2, FIRST_ROW_STEP + 3)
        scalar_operands = [("dz", 0, 0), ("x", 1, 0), ("x", 0, 1), ("x", 1, 1), ("x", 0, 2), ("x", 1, 2), ("dz", 0, 2)]
        scalar_copies = []
        for operand in scalar_operands:
            columns = operand_columns(operand)
            scalar_copies.extend((operand, lo, lo + PIECE) for lo in range(0, columns.stop - columns.start, PIECE))
        w_left = [(pair, g) for pair in range(W_PAIRS) for g in range(GROUPS)]
        dz_complete = set()

        build_table()
        interleave(("x", 0, 0), 0, PIECE, "scalar")
        interleave(("x", 0, 0), PIECE, BANK, "gpsimd")

        for step in range(len(STEPS)):
            before = step - 1
            multiply(step, False)
            if 0 <= step - 2 < SCALAR_EMPTIES_FROM:
                empty_dz(step - 2, "vector")
            waiting = list(due.get(step, []))
            if step > 0:
                if not gpsimd_takes_both(before):
                    upper_half(before, nc.vector)
                turn_dz(before)
            if step > 0 and STEPS[before][0] == B - 1 and groups_done[before]:
                operand = ("dz", B - 1, groups_done[before][0])
                if step == LAST:
                    interleave(operand, PIECE, BANK, "scalar")
                    quantize_features(step - 2)
                    interleave(operand, 0, PIECE, "vector")
                else:
                    interleave(operand, 0, BANK, "vector")
                    quantize_features(step - 2)
                waiting = [operand] + waiting
            else:
                if before >= SCALAR_EMPTIES_FROM:
                    empty_dz(before, "scalar")
                if waiting:
                    quantize_operand(waiting.pop(0))
                if step > 1 and before not in long_steps and step - 2 != KEPT_STEP:
                    quantize_features(step - 2)
            for operand in waiting:
                quantize_operand(operand)
            if step in long_steps:
                quantize_features(before)
            multiply(step, True)
            if step < LAST:
                lower_half(step, nc.gpsimd)
                if gpsimd_takes_both(step):
                    upper_half(step, nc.gpsimd)
            else:
                lower_half(step, nc.vector)
                upper_half(step, nc.vector)

            copies = [copy for copy in scalar_copies if copy[0][0] == "x" or copy[0][1:] in dz_complete]
            copies = copies[:COPIES_PER_STEP]
            scalar_copies = [copy for copy in scalar_copies if copy not in copies]
            dz_complete.update((STEPS[step][0], g) for g in groups_done[step])
            if step >= 2:
                for copy in copies:
                    interleave(*copy, "scalar")
                copies = []
            for pair, g in w_left[:W_BANKS_PER_STEP]:
                empty_w(pair, g, turn_w(pair, g))
                if copies:
                    interleave(*copies.pop(0), "scalar")
            w_left = w_left[W_BANKS_PER_STEP:]
            run_tiles(PASSES_PER_STEP, ["scalar"])

        last_operands = [("dz", b, groups_done[LAST][0]) for b in range(B)]
        turn_dz(LAST)
        free_banks.append(0)
        run_tiles(PASSES_PER_STEP, ["scalar"])
        for operand in last_operands:
            interleave(operand, 0, BANK, "vector")
        for operand in last_operands:
            quantize_operand(operand)
        empty_dz(LAST - 1, "vector")
        empty_dz(LAST, "vector")
        for step in (KEPT_STEP, LAST - 1, LAST):
            quantize_features(step)
        tiles_left[:] = sorted(tiles_left, key=lambda tile: tile[0] == "dx")
        run_tiles(len(tiles_left) * GROUPS, ["vector", "scalar"])
        assert not tiles_left and not scalar_copies and not w_left
